import numpy as np
import ml_dtypes


def mxq(x, axis, fmt="e4m3"):
    dtype, down = {"e4m3": (ml_dtypes.float8_e4m3fn, 7), "e5m2": (ml_dtypes.float8_e5m2, 14)}[fmt]
    v = np.moveaxis(np.asarray(x, np.float32).astype(ml_dtypes.bfloat16).astype(np.float64), axis, -1)
    blocks = v.reshape(v.shape[:-1] + (-1, 32))
    amax = np.abs(blocks).max(-1, keepdims=True)
    byte = np.maximum(np.where(amax > 0, np.frexp(amax)[1] - 1 + 127, 0) - down, 1)
    scale = np.exp2(byte - 127.0)
    codes = (blocks / scale).astype(np.float32).astype(dtype).astype(np.float64)
    return np.moveaxis((codes * scale).reshape(v.shape), -1, axis)


WIDE = False


def mx_kscale(k):
    if not WIDE:
        return np.ones(k)
    levels = np.array([10, -10, 5, -5, 0])
    a = np.random.permutation(np.resize(levels, k // 512 * 4)).reshape(k // 512, 4)
    idx = np.arange(k)
    return np.exp2(a[idx // 512, idx % 128 // 32])


BF16 = ml_dtypes.bfloat16


def bf(x):
    return np.asarray(x, np.float32).astype(BF16)


def f64(x):
    return np.asarray(x).astype(np.float64)


B, S, D = 4, 512, 1024
NB = 2
W = 2 * NB + 1


def setup_inputs():
    s = mx_kscale(D)
    return {"x": bf(np.random.standard_normal((B, S, D)) * s),
            "Wq": bf(np.random.standard_normal((D, D)) / np.sqrt(D) / s[None, :]),
            "bq": bf(np.random.standard_normal(D) * 0.3),
            "k_proj": bf(np.random.standard_normal((B, S, D)))}


def reference(x, Wq, bq, k_proj):
    kf = f64(k_proj)
    q = (mxq(f64(x), 2, "e4m3") @ mxq(f64(Wq), 1, "e4m3").T) + f64(bq)
    scores = np.full((B, S, W), -np.inf)
    for j in range(W):
        o = j - NB
        lo, hi = max(0, -o), S - max(0, o)
        scores[:, lo:hi, j] = (q[:, lo:hi] * kf[:, lo + o:hi + o]).sum(-1) / np.sqrt(D)
    e = np.exp(scores - scores.max(-1, keepdims=True))
    return e / e.sum(-1, keepdims=True)

@@ -1,0 +1,353 @@
+from contextlib import ExitStack
+
+import concourse.mybir as mybir
+from concourse.masks import make_identity
+
+F32 = mybir.dt.float32
+BF16 = mybir.dt.bfloat16
+U32 = mybir.dt.uint32
+U8 = mybir.dt.uint8
+FP8X4 = mybir.dt.float8_e4m3fn_x4
+ALU = mybir.AluOpType
+ACT = mybir.ActivationFunctionType
+AX = mybir.AxisListType
+
+P = 128
+B, S, D = 4, 512, 1024
+W5 = 5
+VB = 1
+PE_BATCHES = (0, 2, 3)
+KPAD = 8
+KW = S + 2 * KPAD
+NWIN = 132
+MOD = 6
+BIG = 1.0e30
+
+FLOPS = 2 * B * S * D * D + 2 * B * S * W5 * D
+
+
+def tile_crosssliceattention_pa_kernel(tc, x, Wq, bq, k_proj, out):
+    nc = tc.nc
+    xf = x.flatten_outer_dims()
+    kf = k_proj.flatten_outer_dims()
+    of = out.flatten_outer_dims()
+
+    with ExitStack() as ctx:
+        consts = ctx.enter_context(tc.tile_pool(name="consts", bufs=1))
+        rawp = ctx.enter_context(tc.tile_pool(name="raw", bufs=1))
+        gp = ctx.enter_context(tc.tile_pool(name="grouped", bufs=2))
+        ktp = ctx.enter_context(tc.tile_pool(name="kt", bufs=2))
+        qtp = ctx.enter_context(tc.tile_pool(name="qt", bufs=2))
+        codes = ctx.enter_context(tc.tile_pool(name="codes", bufs=1))
+        work = ctx.enter_context(tc.tile_pool(name="work", bufs=2))
+        small = ctx.enter_context(tc.tile_pool(name="small", bufs=1))
+        tp = ctx.enter_context(tc.psum_pool(name="tp", bufs=2))
+        mxp = ctx.enter_context(tc.psum_pool(name="mx", bufs=3))
+        sp = ctx.enter_context(tc.psum_pool(name="sps", bufs=2))
+
+        w_raw = rawp.tile([P, 4, 2, D], BF16, tag="big")
+        wv = Wq.rearrange("(u p e) i -> p u e i", p=P, e=2)
+        for u in range(4):
+            nc.sync.dma_start(out=w_raw[:, u, :, :], in_=wv[:, u, :, :])
+
+        bb = consts.tile([P, D], BF16)
+        nc.scalar.dma_start(out=bb[:], in_=bq.partition_broadcast(P))
+        bpp_bf = consts.tile([P, 4, 2], BF16)
+        nc.scalar.dma_start(out=bpp_bf[:], in_=bq.rearrange("(u p e) -> p u e", p=P, e=2))
+
+        xraw = {}
+        kraw = {}
+
+        def load_x(b):
+            xr = rawp.tile([P, 4, D], BF16, name="xraw%d" % b)
+            rows = xf[S * b : S * (b + 1), :]
+            if b == VB:
+                view = rows.rearrange("(p r) i -> p r i", r=4)
+            else:
+                view = rows.rearrange("(t p) i -> p t i", p=P)
+            for hh in range(2):
+                nc.sync.dma_start(out=xr[:, 2 * hh : 2 * hh + 2, :], in_=view[:, 2 * hh : 2 * hh + 2, :])
+            xraw[b] = xr
+
+        def load_k(b):
+            kr = rawp.tile([P, 4, D], BF16, name="kraw%d" % b)
+            view = kf[S * b : S * (b + 1), :].rearrange("(t p) d -> p t d", p=P)
+            for hh in range(2):
+                nc.sync.dma_start(out=kr[:, 2 * hh : 2 * hh + 2, :], in_=view[:, 2 * hh : 2 * hh + 2, :])
+            kraw[b] = kr
+
+        load_x(VB)
+        load_x(0)
+        load_k(0)
+        k_v = rawp.tile([P, 8, D], BF16)
+        base = S * VB - 2
+        for hh in range(2):
+            nc.sync.dma_start(
+                out=k_v[:, 4 * hh : 4 * hh + 4, :],
+                in_=kf[base + 4 * hh : base + 4 * hh + S, :].rearrange("(p c) d -> p c d", c=4),
+            )
+        load_x(2)
+        load_k(2)
+        load_x(3)
+        load_k(3)
+
+        ident = consts.tile([P, P], F32)
+        make_identity(nc, ident[:])
+        warm = consts.tile([P, 1], F32)
+        nc.vector.memset(warm[:], 0.0)
+        warm2 = consts.tile([P, 1], F32)
+        nc.scalar.activation(out=warm2[:], in_=warm[:], func=ACT.Exp)
+
+        band = consts.tile([P, NWIN], F32)
+        nc.vector.memset(band[:], 0.0)
+        for j in range(W5):
+            nc.vector.tensor_tensor(out=band[:, j : j + P], in0=band[:, j : j + P], in1=ident[:], op=ALU.add)
+        idw = consts.tile([P, NWIN], F32)
+        nc.vector.memset(idw[:], 0.0)
+        nc.vector.tensor_copy(out=idw[:, 0:P], in_=ident[:])
+        ind = consts.tile([P, MOD], F32)
+        nc.vector.tensor_reduce(out=ind[:], in_=idw[:].rearrange("p (m r) -> p r m", r=MOD), axis=AX.X, op=ALU.add)
+
+        neg4 = consts.tile([P, 4, W5], F32)
+        nc.vector.memset(neg4[:], 0.0)
+        nc.vector.tensor_scalar_mul(out=neg4[:, 0, 0:2], in0=ident[:, 0:1].to_broadcast([P, 2]), scalar1=-BIG)
+        nc.vector.scalar_tensor_tensor(
+            out=neg4[:, 0, 0:1], in0=ident[:, 1:2], scalar=-BIG, in1=neg4[:, 0, 0:1], op0=ALU.mult, op1=ALU.add
+        )
+        nc.vector.tensor_scalar_mul(out=neg4[:, 3, 3:5], in0=ident[:, 127:128].to_broadcast([P, 2]), scalar1=-BIG)
+        nc.vector.scalar_tensor_tensor(
+            out=neg4[:, 3, 4:5], in0=ident[:, 126:127], scalar=-BIG, in1=neg4[:, 3, 4:5], op0=ALU.mult, op1=ALU.add
+        )
+        negv = consts.tile([P, 4, W5], F32)
+        nc.vector.memset(negv[:], 0.0)
+        nc.vector.tensor_scalar_mul(out=negv[:, 0, 0:2], in0=ident[:, 0:1].to_broadcast([P, 2]), scalar1=-BIG)
+        nc.vector.tensor_scalar_mul(out=negv[:, 1, 0:1], in0=ident[:, 0:1], scalar1=-BIG)
+        nc.vector.tensor_scalar_mul(out=negv[:, 3, 3:5], in0=ident[:, 127:128].to_broadcast([P, 2]), scalar1=-BIG)
+        nc.vector.tensor_scalar_mul(out=negv[:, 2, 4:5], in0=ident[:, 127:128], scalar1=-BIG)
+
+        bpp = consts.tile([P, 8], F32)
+        nc.vector.tensor_copy(out=bpp[:], in_=bpp_bf[:].rearrange("p u e -> p (u e)"))
+
+        rr = small.tile([P, 16, MOD + W5], F32)
+        nc.vector.memset(rr[:], 0.0)
+        ypad = small.tile([P, W5, P], F32)
+        nc.vector.memset(ypad[:], 0.0)
+
+        turn = [0]
+
+        def evac(out_ap, in_ap, share):
+            turn[0] += 1
+            if share and turn[0] % 2 == 0:
+                nc.vector.tensor_copy(out=out_ap, in_=in_ap)
+            else:
+                nc.scalar.copy(out=out_ap, in_=in_ap)
+
+        def transpose_words(words):
+            bank = tp.tile([P, 4, P], F32, tag="tp")
+            for blk in range(4):
+                nc.tensor.transpose(bank[:, blk, :], words[:, P * blk : P * (blk + 1)], ident[:])
+            return bank
+
+        wc = codes.tile([P, 2, D], U32, align_bytes=64)
+        ws = codes.tile([P, 2, D], U8, align_bytes=64)
+        xc = {}
+        xs = {}
+
+        def stage_w():
+            gw = ktp.tile([P, 2, 4 * D], BF16, tag="kt", align_bytes=64)
+            gwf = gw[:].bitcast(F32).rearrange("p g (c u) -> p g c u", u=2)
+            ww = w_raw[:].bitcast(F32)
+            for c in range(8):
+                bank = transpose_words(ww[:, c // 2, c % 2, :])
+                evac(gwf[:, :, P * c : P * (c + 1), :], bank[:].rearrange("p (g u) c -> p g c u", u=2), True)
+                if c % 4 == 3:
+                    h = c // 4
+                    for g in range(2):
+                        nc.vector.quantize_mx(
+                            out=wc[:, g, 512 * h : 512 * (h + 1)].bitcast(FP8X4),
+                            scales=ws[:, g, 512 * h : 512 * (h + 1)],
+                            in_=gw[:, g, 2048 * h : 2048 * (h + 1)],
+                        )
+
+        def stage_x(b, share):
+            grp = gp.tile([P, 2, 4 * S], BF16, tag="g", align_bytes=64)
+            gf = grp[:].bitcast(F32).rearrange("p g (c u) -> p g c u", u=2)
+            xw = xraw[b][:].bitcast(F32)
+            for j in range(4):
+                bank = transpose_words(xw[:, j, :])
+                evac(gf[:, :, P * j : P * (j + 1), :], bank[:].rearrange("p (g u) c -> p g c u", u=2), share)
+            xcb = codes.tile([P, 2, S], U32, name="xc%d" % b, align_bytes=64)
+            xsb = codes.tile([P, 2, S], U8, name="xs%d" % b, align_bytes=64)
+            for g in range(2):
+                nc.vector.quantize_mx(out=xcb[:, g, :].bitcast(FP8X4), scales=xsb[:, g, :], in_=grp[:, g, :])
+            xc[b] = xcb
+            xs[b] = xsb
+
+        kts = {}
+        qts = {}
+
+        def stage_k(b, share):
+            kt = ktp.tile([P, 8, KW], F32, tag="kt", align_bytes=64)
+            nc.gpsimd.memset(kt[:, :, 0:KPAD], 0.0)
+            nc.gpsimd.memset(kt[:, :, KPAD + S : KW], 0.0)
+            kw = kraw[b][:].bitcast(F32)
+            for tb in range(4):
+                bank = transpose_words(kw[:, tb, :])
+                lo = KPAD + P * tb
+                evac(
+                    kt[:, :, lo : lo + P].rearrange("p (u e) k -> p u e k", e=2),
+                    bank[:].bitcast(BF16).rearrange("p u (k e) -> p u e k", e=2),
+                    share,
+                )
+            kts[b] = kt
+
+        scv = small.tile([P, 4, W5], F32)
+
+        def mx_v():
+            for r in range(4):
+                for h in range(2):
+                    qv = mxp.tile([P, 512], F32, tag="mx")
+                    for g in range(2):
+                        nc.tensor.matmul_mx(
+                            out=qv[:],
+                            lhsT=xc[VB][:, g, P * r : P * (r + 1)].bitcast(FP8X4),
+                            lhsT_scale=xs[VB][:, g, P * r : P * (r + 1)],
+                            rhs=wc[:, g, 512 * h : 512 * (h + 1)].bitcast(FP8X4),
+                            rhs_scale=ws[:, g, 512 * h : 512 * (h + 1)],
+                            start=(g == 0),
+                            stop=(g == 1),
+                        )
+                    nc.vector.tensor_tensor(
+                        out=qb[:, r, 512 * h : 512 * (h + 1)].rearrange("p (u q e) -> p u q e", u=2, e=2),
+                        in0=qv[:].rearrange("p (u e q) -> p u q e", u=2, e=2),
+                        in1=bb[:, 512 * h : 512 * (h + 1)].rearrange("p (u q e) -> p u q e", u=2, e=2),
+                        op=ALU.add,
+                    )
+
+        def v_scores(r):
+            for j in range(W5):
+                junk = work.tile([P, D], F32, tag="junk", bufs=1)
+                nc.vector.scalar_tensor_tensor(
+                    out=junk[:],
+                    in0=qb[:, r, :],
+                    scalar=1.0,
+                    in1=k_v[:, r + j, :],
+                    op0=ALU.mult,
+                    op1=ALU.mult,
+                    accum_out=scv[:, r, j : j + 1],
+                )
+
+        def mx_pe(b):
+            qt_sb = qtp.tile([P, 8, S], F32, tag="qt")
+            for c in range(8):
+                qt = mxp.tile([P, 512], F32, tag="mx")
+                for g in range(2):
+                    nc.tensor.matmul_mx(
+                        out=qt[:],
+                        lhsT=wc[:, g, P * c : P * (c + 1)].bitcast(FP8X4),
+                        lhsT_scale=ws[:, g, P * c : P * (c + 1)],
+                        rhs=xc[b][:, g, :].bitcast(FP8X4),
+                        rhs_scale=xs[b][:, g, :],
+                        start=(g == 0),
+                        stop=(g == 1),
+                    )
+                nc.scalar.activation(out=qt_sb[:, c, :], in_=qt[:], func=ACT.Identity, bias=bpp[:, c : c + 1], scale=1.0)
+            qts[b] = qt_sb
+
+        def scores_pe(b):
+            for half in range(2):
+                sps = sp.tile([P, 2, NWIN], F32, tag="s")
+                for ti in range(2):
+                    tb = 2 * half + ti
+                    lo = KPAD - 2 + P * tb
+                    for c in range(8):
+                        nc.tensor.matmul(
+                            out=sps[:, ti, :],
+                            lhsT=qts[b][:, c, P * tb : P * (tb + 1)],
+                            rhs=kts[b][:, c, lo : lo + NWIN],
+                            start=(c == 0),
+                            stop=(c == 7),
+                        )
+                bm = work.tile([P, 2, NWIN], F32, tag="bm")
+                nc.vector.tensor_tensor(
+                    out=bm[:], in0=sps[:], in1=band[:].unsqueeze(1).to_broadcast([P, 2, NWIN]), op=ALU.mult
+                )
+                slot = 4 * b + 2 * half
+                nc.vector.tensor_reduce(
+                    out=rr[:, slot : slot + 2, 0:MOD],
+                    in_=bm[:].rearrange("p t (m r) -> p t r m", r=MOD),
+                    axis=AX.X,
+                    op=ALU.add,
+                )
+
+        def softmax(sc, groups, dest, label):
+            mx = small.tile([P, groups], F32, name="mx" + label)
+            nc.vector.tensor_reduce(out=mx[:], in_=sc[:], axis=AX.X, op=ALU.max)
+            nc.vector.tensor_tensor(
+                out=sc[:], in0=sc[:], in1=mx[:].unsqueeze(2).to_broadcast([P, groups, W5]), op=ALU.subtract
+            )
+            ex = small.tile([P, groups, W5], F32, name="ex" + label)
+            nc.scalar.activation(out=ex[:], in_=sc[:], func=ACT.Exp, scale=1.0 / 32.0)
+            sm = small.tile([P, groups], F32, name="sm" + label)
+            nc.vector.tensor_reduce(out=sm[:], in_=ex[:], axis=AX.X, op=ALU.add)
+            rs = small.tile([P, groups], F32, name="rs" + label)
+            nc.vector.reciprocal(out=rs[:], in_=sm[:])
+            nc.vector.tensor_tensor(
+                out=dest, in0=ex[:], in1=rs[:].unsqueeze(2).to_broadcast([P, groups, W5]), op=ALU.mult
+            )
+
+        stage_w()
+        stage_x(VB, True)
+        stage_x(0, True)
+        stage_k(0, True)
+        qb = rawp.tile([P, 4, D], F32, tag="big")
+        mx_v()
+        mx_pe(0)
+        v_scores(0)
+        stage_x(2, False)
+        stage_k(2, False)
+        scores_pe(0)
+        v_scores(1)
+        mx_pe(2)
+        stage_x(3, False)
+        stage_k(3, False)
+        v_scores(2)
+        scores_pe(2)
+        mx_pe(3)
+        v_scores(3)
+        nc.vector.tensor_tensor(out=scv[:], in0=scv[:], in1=negv[:], op=ALU.add)
+        yv = small.tile([P, 4, W5], F32)
+        softmax(scv, 4, yv[:], "v")
+        nc.sync.dma_start(
+            out=of[S * VB : S * (VB + 1), :].rearrange("(p r) j -> p (r j)", r=4),
+            in_=yv[:].rearrange("p r j -> p (r j)"),
+        )
+        scores_pe(3)
+
+        nc.vector.tensor_copy(out=rr[:, :, MOD : MOD + W5], in_=rr[:, :, 0:W5])
+        sc = small.tile([P, 16, W5], F32)
+        nc.vector.tensor_scalar_mul(out=sc[:], in0=rr[:, :, 0:W5], scalar1=ind[:, 0:1])
+        for rho in range(1, MOD):
+            nc.vector.scalar_tensor_tensor(
+                out=sc[:], in0=rr[:, :, rho : rho + W5], scalar=ind[:, rho : rho + 1], in1=sc[:], op0=ALU.mult, op1=ALU.add
+            )
+        scb = sc[:].rearrange("p (b t) j -> p b (t j)", b=4)
+        nc.vector.tensor_tensor(
+            out=scb,
+            in0=scb,
+            in1=neg4[:].rearrange("p t j -> p (t j)").unsqueeze(1).to_broadcast([P, 4, 4 * W5]),
+            op=ALU.add,
+        )
+        softmax(sc, 16, ypad[:, :, 0:16].rearrange("p j t -> p t j"), "p")
+
+        ta = tp.tile([P, 4, P], F32, tag="tp")
+        for j in range(4):
+            nc.tensor.transpose(ta[:, j, :], ypad[:, j, :], ident[:])
+        tb4 = tp.tile([P, 4, P], F32, tag="tp")
+        nc.tensor.transpose(tb4[:, 0, :], ypad[:, 4, :], ident[:])
+        z2 = small.tile([P, P, W5], F32)
+        nc.vector.tensor_copy(out=z2[:, :, 0:4], in_=ta[:].rearrange("s j p -> s p j"))
+        nc.vector.tensor_copy(out=z2[:, :, 4:5], in_=tb4[:, 0:1, :].rearrange("s j p -> s p j"))
+        ov = of.rearrange("(t p) j -> t (p j)", p=P)
+        nc.sync.dma_start(out=ov[0:4, :], in_=z2[0:4, :, :].rearrange("s p j -> s (p j)"))
+        nc.sync.dma_start(out=ov[8:16, :], in_=z2[8:16, :, :].rearrange("s p j -> s (p j)"))

@@ -15,8 +15,9 @@ AX = mybir.AxisListType
 P = 128
 B, S, D = 4, 512, 1024
 W5 = 5
-VB = 1
-PE_BATCHES = (0, 2, 3)
+NV = 4
+VS = 512
+PE_BATCHES = tuple([b for b in range(B) if not VS <= S * b < VS + P * NV])
 KPAD = 8
 KW = S + 2 * KPAD
 NWIN = 132
@@ -41,33 +42,35 @@ def tile_crosssliceattention_pa_kernel(tc, x, Wq, bq, k_proj, out):
         codes = ctx.enter_context(tc.tile_pool(name="codes", bufs=1))
         work = ctx.enter_context(tc.tile_pool(name="work", bufs=2))
         small = ctx.enter_context(tc.tile_pool(name="small", bufs=1))
-        tp = ctx.enter_context(tc.psum_pool(name="tp", bufs=2))
+        tp = ctx.enter_context(tc.psum_pool(name="tp", bufs=3))
         mxp = ctx.enter_context(tc.psum_pool(name="mx", bufs=3))
         sp = ctx.enter_context(tc.psum_pool(name="sps", bufs=2))
+        ctx.enter_context(tc.manual_schedule())
+
+        brow = consts.tile([P, 2 * P], BF16)
+        nc.vector.memset(brow[:], 0.0)
+        nc.sync.dma_start(out=brow[0:4, :], in_=bq.rearrange("(u w) -> u w", u=4))
 
         w_raw = rawp.tile([P, 4, 2, D], BF16, tag="big")
         wv = Wq.rearrange("(u p e) i -> p u e i", p=P, e=2)
-        for u in range(4):
-            nc.sync.dma_start(out=w_raw[:, u, :, :], in_=wv[:, u, :, :])
-
-        bb = consts.tile([P, D], BF16)
-        nc.scalar.dma_start(out=bb[:], in_=bq.partition_broadcast(P))
-        bpp_bf = consts.tile([P, 4, 2], BF16)
-        nc.scalar.dma_start(out=bpp_bf[:], in_=bq.rearrange("(u p e) -> p u e", p=P, e=2))
-
         xraw = {}
         kraw = {}
 
-        def load_x(b):
-            xr = rawp.tile([P, 4, D], BF16, name="xraw%d" % b)
-            rows = xf[S * b : S * (b + 1), :]
-            if b == VB:
-                view = rows.rearrange("(p r) i -> p r i", r=4)
-            else:
-                view = rows.rearrange("(t p) i -> p t i", p=P)
+        def load_w(u):
+            nc.sync.dma_start(out=w_raw[:, u, :, :], in_=wv[:, u, :, :])
+
+        def load_x(key, view):
+            xr = rawp.tile([P, 4, D], BF16, tag="xr", bufs=3)
             for hh in range(2):
                 nc.sync.dma_start(out=xr[:, 2 * hh : 2 * hh + 2, :], in_=view[:, 2 * hh : 2 * hh + 2, :])
-            xraw[b] = xr
+            xraw[key] = xr
+
+        def load_xv(vg):
+            view = xf[VS : VS + P * NV, :].rearrange("(p r) i -> p r i", r=NV)
+            load_x("v%d" % vg, view[:, 4 * vg : 4 * vg + 4, :])
+
+        def load_xp(b):
+            load_x("p%d" % b, xf[S * b : S * (b + 1), :].rearrange("(t p) i -> p t i", p=P))
 
         def load_k(b):
             kr = rawp.tile([P, 4, D], BF16, name="kraw%d" % b)
@@ -76,68 +79,100 @@ def tile_crosssliceattention_pa_kernel(tc, x, Wq, bq, k_proj, out):
                 nc.sync.dma_start(out=kr[:, 2 * hh : 2 * hh + 2, :], in_=view[:, 2 * hh : 2 * hh + 2, :])
             kraw[b] = kr
 
-        load_x(VB)
-        load_x(0)
-        load_k(0)
-        k_v = rawp.tile([P, 8, D], BF16)
-        base = S * VB - 2
-        for hh in range(2):
-            nc.sync.dma_start(
-                out=k_v[:, 4 * hh : 4 * hh + 4, :],
-                in_=kf[base + 4 * hh : base + 4 * hh + S, :].rearrange("(p c) d -> p c d", c=4),
-            )
-        load_x(2)
-        load_k(2)
-        load_x(3)
-        load_k(3)
+        load_w(0)
+        load_w(1)
+        load_xv(0)
+        load_w(2)
+        load_w(3)
+        for vg in range(1, NV // 4):
+            load_xv(vg)
+        load_xp(PE_BATCHES[0])
+        load_k(PE_BATCHES[0])
+        k_v = rawp.tile([P, NV + 4, D], BF16)
+        base = VS - 2
+        nc.sync.dma_start(
+            out=k_v[:, 0:NV, :], in_=kf[base : base + P * NV, :].rearrange("(p c) d -> p c d", c=NV)
+        )
+        nc.sync.dma_start(
+            out=k_v[:, NV : NV + 4, :],
+            in_=kf[base + NV : base + NV + P * NV, :].rearrange("(p c) d -> p c d", c=NV)[:, 0:4, :],
+        )
+        for b in PE_BATCHES[1:-1]:
+            load_xp(b)
+            load_k(b)
 
         ident = consts.tile([P, P], F32)
         make_identity(nc, ident[:])
         warm = consts.tile([P, 1], F32)
-        nc.vector.memset(warm[:], 0.0)
+        nc.gpsimd.memset(warm[:], 0.0)
         warm2 = consts.tile([P, 1], F32)
         nc.scalar.activation(out=warm2[:], in_=warm[:], func=ACT.Exp)
-
         band = consts.tile([P, NWIN], F32)
-        nc.vector.memset(band[:], 0.0)
-        for j in range(W5):
-            nc.vector.tensor_tensor(out=band[:, j : j + P], in0=band[:, j : j + P], in1=ident[:], op=ALU.add)
+        nc.gpsimd.memset(band[:], 0.0)
         idw = consts.tile([P, NWIN], F32)
-        nc.vector.memset(idw[:], 0.0)
-        nc.vector.tensor_copy(out=idw[:, 0:P], in_=ident[:])
-        ind = consts.tile([P, MOD], F32)
-        nc.vector.tensor_reduce(out=ind[:], in_=idw[:].rearrange("p (m r) -> p r m", r=MOD), axis=AX.X, op=ALU.add)
-
+        nc.gpsimd.memset(idw[:], 0.0)
         neg4 = consts.tile([P, 4, W5], F32)
-        nc.vector.memset(neg4[:], 0.0)
-        nc.vector.tensor_scalar_mul(out=neg4[:, 0, 0:2], in0=ident[:, 0:1].to_broadcast([P, 2]), scalar1=-BIG)
-        nc.vector.scalar_tensor_tensor(
-            out=neg4[:, 0, 0:1], in0=ident[:, 1:2], scalar=-BIG, in1=neg4[:, 0, 0:1], op0=ALU.mult, op1=ALU.add
-        )
-        nc.vector.tensor_scalar_mul(out=neg4[:, 3, 3:5], in0=ident[:, 127:128].to_broadcast([P, 2]), scalar1=-BIG)
-        nc.vector.scalar_tensor_tensor(
-            out=neg4[:, 3, 4:5], in0=ident[:, 126:127], scalar=-BIG, in1=neg4[:, 3, 4:5], op0=ALU.mult, op1=ALU.add
-        )
-        negv = consts.tile([P, 4, W5], F32)
-        nc.vector.memset(negv[:], 0.0)
-        nc.vector.tensor_scalar_mul(out=negv[:, 0, 0:2], in0=ident[:, 0:1].to_broadcast([P, 2]), scalar1=-BIG)
-        nc.vector.tensor_scalar_mul(out=negv[:, 1, 0:1], in0=ident[:, 0:1], scalar1=-BIG)
-        nc.vector.tensor_scalar_mul(out=negv[:, 3, 3:5], in0=ident[:, 127:128].to_broadcast([P, 2]), scalar1=-BIG)
-        nc.vector.tensor_scalar_mul(out=negv[:, 2, 4:5], in0=ident[:, 127:128], scalar1=-BIG)
-
-        bpp = consts.tile([P, 8], F32)
-        nc.vector.tensor_copy(out=bpp[:], in_=bpp_bf[:].rearrange("p u e -> p (u e)"))
-
+        nc.gpsimd.memset(neg4[:], 0.0)
+        negv = consts.tile([P, NV, W5], F32)
+        nc.gpsimd.memset(negv[:], 0.0)
         rr = small.tile([P, 16, MOD + W5], F32)
-        nc.vector.memset(rr[:], 0.0)
+        nc.gpsimd.memset(rr[:], 0.0)
         ypad = small.tile([P, W5, P], F32)
-        nc.vector.memset(ypad[:], 0.0)
+        nc.gpsimd.memset(ypad[:], 0.0)
 
-        turn = [0]
+        bt = tp.tile([P, 4, P], F32, tag="tp")
+        nc.tensor.transpose(bt[:, 0, :], brow[:].bitcast(F32), ident[:])
+        bw = consts.tile([P, 4], F32)
+        nc.vector.tensor_copy(out=bw[:], in_=bt[:, 0, 0:4])
+        rep = consts.tile([P, 4, P], F32)
+        nc.vector.tensor_copy(out=rep[:], in_=bw[:].unsqueeze(2).to_broadcast([P, 4, P]))
+        bbank = tp.tile([P, 4, P], F32, tag="tp")
+        for u in range(4):
+            nc.tensor.transpose(bbank[:, u, :], rep[:, u, :], ident[:])
+        bb = consts.tile([P, D], BF16)
+        nc.vector.tensor_copy(out=bb[:].bitcast(F32), in_=bbank[:].rearrange("p u w -> p (u w)"))
+        bpp = consts.tile([P, 8], F32)
+        nc.vector.tensor_copy(out=bpp[:], in_=bw[:].bitcast(BF16))
 
-        def evac(out_ap, in_ap, share):
-            turn[0] += 1
-            if share and turn[0] % 2 == 0:
+        def late_consts():
+            for j in range(W5):
+                nc.vector.tensor_tensor(out=band[:, j : j + P], in0=band[:, j : j + P], in1=ident[:], op=ALU.add)
+            nc.vector.tensor_copy(out=idw[:, 0:P], in_=ident[:])
+            nc.vector.tensor_reduce(
+                out=ind[:], in_=idw[:].rearrange("p (m r) -> p r m", r=MOD), axis=AX.X, op=ALU.add
+            )
+            for tb, j, p in ((0, 0, 0), (0, 1, 0), (0, 0, 1), (3, 3, 127), (3, 4, 127), (3, 4, 126)):
+                nc.vector.scalar_tensor_tensor(
+                    out=neg4[:, tb, j : j + 1],
+                    in0=ident[:, p : p + 1],
+                    scalar=-BIG,
+                    in1=neg4[:, tb, j : j + 1],
+                    op0=ALU.mult,
+                    op1=ALU.add,
+                )
+            nc.vector.tensor_copy(
+                out=negfull[:].rearrange("p (b t) j -> p b (t j)", b=4),
+                in_=neg4[:].rearrange("p t j -> p (t j)").unsqueeze(1).to_broadcast([P, 4, 4 * W5]),
+            )
+            for p in range(P):
+                for r in range(NV):
+                    tok = VS + NV * p + r
+                    for j in range(W5):
+                        if (tok + j - 2) // S != tok // S:
+                            nc.vector.scalar_tensor_tensor(
+                                out=negv[:, r, j : j + 1],
+                                in0=ident[:, p : p + 1],
+                                scalar=-BIG,
+                                in1=negv[:, r, j : j + 1],
+                                op0=ALU.mult,
+                                op1=ALU.add,
+                            )
+
+        ind = consts.tile([P, MOD], F32)
+        negfull = consts.tile([P, 16, W5], F32)
+
+        def evac(eng, out_ap, in_ap):
+            if eng == "v":
                 nc.vector.tensor_copy(out=out_ap, in_=in_ap)
             else:
                 nc.scalar.copy(out=out_ap, in_=in_ap)
@@ -150,82 +185,103 @@ def tile_crosssliceattention_pa_kernel(tc, x, Wq, bq, k_proj, out):
 
         wc = codes.tile([P, 2, D], U32, align_bytes=64)
         ws = codes.tile([P, 2, D], U8, align_bytes=64)
+        gw = ktp.tile([P, 2, 4 * D], BF16, tag="kt", align_bytes=64)
+        gwf = gw[:].bitcast(F32).rearrange("p g (c u) -> p g c u", u=2)
+        ww = w_raw[:].bitcast(F32)
         xc = {}
         xs = {}
-
-        def stage_w():
-            gw = ktp.tile([P, 2, 4 * D], BF16, tag="kt", align_bytes=64)
-            gwf = gw[:].bitcast(F32).rearrange("p g (c u) -> p g c u", u=2)
-            ww = w_raw[:].bitcast(F32)
-            for c in range(8):
-                bank = transpose_words(ww[:, c // 2, c % 2, :])
-                evac(gwf[:, :, P * c : P * (c + 1), :], bank[:].rearrange("p (g u) c -> p g c u", u=2), True)
-                if c % 4 == 3:
-                    h = c // 4
-                    for g in range(2):
-                        nc.vector.quantize_mx(
-                            out=wc[:, g, 512 * h : 512 * (h + 1)].bitcast(FP8X4),
-                            scales=ws[:, g, 512 * h : 512 * (h + 1)],
-                            in_=gw[:, g, 2048 * h : 2048 * (h + 1)],
-                        )
-
-        def stage_x(b, share):
-            grp = gp.tile([P, 2, 4 * S], BF16, tag="g", align_bytes=64)
-            gf = grp[:].bitcast(F32).rearrange("p g (c u) -> p g c u", u=2)
-            xw = xraw[b][:].bitcast(F32)
-            for j in range(4):
-                bank = transpose_words(xw[:, j, :])
-                evac(gf[:, :, P * j : P * (j + 1), :], bank[:].rearrange("p (g u) c -> p g c u", u=2), share)
-            xcb = codes.tile([P, 2, S], U32, name="xc%d" % b, align_bytes=64)
-            xsb = codes.tile([P, 2, S], U8, name="xs%d" % b, align_bytes=64)
-            for g in range(2):
-                nc.vector.quantize_mx(out=xcb[:, g, :].bitcast(FP8X4), scales=xsb[:, g, :], in_=grp[:, g, :])
-            xc[b] = xcb
-            xs[b] = xsb
-
+        grp = {}
         kts = {}
         qts = {}
+        spt = {}
 
-        def stage_k(b, share):
-            kt = ktp.tile([P, 8, KW], F32, tag="kt", align_bytes=64)
-            nc.gpsimd.memset(kt[:, :, 0:KPAD], 0.0)
-            nc.gpsimd.memset(kt[:, :, KPAD + S : KW], 0.0)
-            kw = kraw[b][:].bitcast(F32)
-            for tb in range(4):
-                bank = transpose_words(kw[:, tb, :])
-                lo = KPAD + P * tb
-                evac(
-                    kt[:, :, lo : lo + P].rearrange("p (u e) k -> p u e k", e=2),
-                    bank[:].bitcast(BF16).rearrange("p u (k e) -> p u e k", e=2),
-                    share,
+        def w_bank(c, eng):
+            bank = transpose_words(ww[:, c // 2, c % 2, :])
+            evac(eng, gwf[:, :, P * c : P * (c + 1), :], bank[:].rearrange("p (g u) c -> p g c u", u=2))
+
+        def w_quant(h):
+            for g in range(2):
+                nc.vector.quantize_mx(
+                    out=wc[:, g, 512 * h : 512 * (h + 1)].bitcast(FP8X4),
+                    scales=ws[:, g, 512 * h : 512 * (h + 1)],
+                    in_=gw[:, g, 2048 * h : 2048 * (h + 1)],
                 )
-            kts[b] = kt
 
-        scv = small.tile([P, 4, W5], F32)
+        def x_bank(key, j, eng):
+            if j == 0:
+                gt = gp.tile([P, 2, 4 * S], BF16, tag="g", align_bytes=64)
+                grp[key] = gt
+            gf = grp[key][:].bitcast(F32).rearrange("p g (c u) -> p g c u", u=2)
+            bank = transpose_words(xraw[key][:].bitcast(F32)[:, j, :])
+            evac(eng, gf[:, :, P * j : P * (j + 1), :], bank[:].rearrange("p (g u) c -> p g c u", u=2))
 
-        def mx_v():
-            for r in range(4):
-                for h in range(2):
-                    qv = mxp.tile([P, 512], F32, tag="mx")
-                    for g in range(2):
-                        nc.tensor.matmul_mx(
-                            out=qv[:],
-                            lhsT=xc[VB][:, g, P * r : P * (r + 1)].bitcast(FP8X4),
-                            lhsT_scale=xs[VB][:, g, P * r : P * (r + 1)],
-                            rhs=wc[:, g, 512 * h : 512 * (h + 1)].bitcast(FP8X4),
-                            rhs_scale=ws[:, g, 512 * h : 512 * (h + 1)],
-                            start=(g == 0),
-                            stop=(g == 1),
-                        )
-                    nc.vector.tensor_tensor(
-                        out=qb[:, r, 512 * h : 512 * (h + 1)].rearrange("p (u q e) -> p u q e", u=2, e=2),
-                        in0=qv[:].rearrange("p (u e q) -> p u q e", u=2, e=2),
-                        in1=bb[:, 512 * h : 512 * (h + 1)].rearrange("p (u q e) -> p u q e", u=2, e=2),
-                        op=ALU.add,
-                    )
+        def x_quant(key):
+            xcb = codes.tile([P, 2, S], U32, name="xc" + key, align_bytes=64)
+            xsb = codes.tile([P, 2, S], U8, name="xs" + key, align_bytes=64)
+            for g in range(2):
+                nc.vector.quantize_mx(out=xcb[:, g, :].bitcast(FP8X4), scales=xsb[:, g, :], in_=grp[key][:, g, :])
+            xc[key] = xcb
+            xs[key] = xsb
 
-        def v_scores(r):
-            for j in range(W5):
+        def k_bank(b, tb, eng):
+            if tb == 0:
+                kt = ktp.tile([P, 8, KW], F32, tag="kt", align_bytes=64)
+                nc.gpsimd.memset(kt[:, :, 0:KPAD], 0.0)
+                nc.gpsimd.memset(kt[:, :, KPAD + S : KW], 0.0)
+                kts[b] = kt
+            bank = transpose_words(kraw[b][:].bitcast(F32)[:, tb, :])
+            lo = KPAD + P * tb
+            evac(
+                eng,
+                kts[b][:, :, lo : lo + P].rearrange("p (u e) k -> p u e k", e=2),
+                bank[:].bitcast(BF16).rearrange("p u (k e) -> p u e k", e=2),
+            )
+
+        scv = small.tile([P, NV, W5], F32)
+        vdone = [0]
+
+        def mxv_group(r, h):
+            key = "v%d" % (r // 4)
+            cols = slice(P * (r % 4), P * (r % 4 + 1))
+            qv = mxp.tile([P, 512], F32, tag="mx")
+            for g in range(2):
+                nc.tensor.matmul_mx(
+                    out=qv[:],
+                    lhsT=xc[key][:, g, cols].bitcast(FP8X4),
+                    lhsT_scale=xs[key][:, g, cols],
+                    rhs=wc[:, g, 512 * h : 512 * (h + 1)].bitcast(FP8X4),
+                    rhs_scale=ws[:, g, 512 * h : 512 * (h + 1)],
+                    start=(g == 0),
+                    stop=(g == 1),
+                )
+            nc.vector.tensor_tensor(
+                out=qb[:, r, 512 * h : 512 * (h + 1)].rearrange("p (u q e) -> p u q e", u=2, e=2),
+                in0=qv[:].rearrange("p (u e q) -> p u q e", u=2, e=2),
+                in1=bb[:, 512 * h : 512 * (h + 1)].rearrange("p (u q e) -> p u q e", u=2, e=2),
+                op=ALU.add,
+            )
+
+        def softmax(sc_t, groups, dest, label):
+            mx = small.tile([P, groups], F32, name="mx" + label)
+            nc.vector.tensor_reduce(out=mx[:], in_=sc_t[:], axis=AX.X, op=ALU.max)
+            nc.vector.tensor_tensor(
+                out=sc_t[:], in0=sc_t[:], in1=mx[:].unsqueeze(2).to_broadcast([P, groups, W5]), op=ALU.subtract
+            )
+            ex = small.tile([P, groups, W5], F32, name="ex" + label)
+            nc.scalar.activation(out=ex[:], in_=sc_t[:], func=ACT.Exp, scale=1.0 / 32.0)
+            sm = small.tile([P, groups], F32, name="sm" + label)
+            nc.vector.tensor_reduce(out=sm[:], in_=ex[:], axis=AX.X, op=ALU.add)
+            rs = small.tile([P, groups], F32, name="rs" + label)
+            nc.vector.reciprocal(out=rs[:], in_=sm[:])
+            nc.vector.tensor_tensor(
+                out=dest, in0=ex[:], in1=rs[:].unsqueeze(2).to_broadcast([P, groups, W5]), op=ALU.mult
+            )
+
+        def vfill(n):
+            for i in range(n):
+                if vdone[0] >= W5 * NV:
+                    return
+                r, j = divmod(vdone[0], W5)
                 junk = work.tile([P, D], F32, tag="junk", bufs=1)
                 nc.vector.scalar_tensor_tensor(
                     out=junk[:],
@@ -236,109 +292,137 @@ def tile_crosssliceattention_pa_kernel(tc, x, Wq, bq, k_proj, out):
                     op1=ALU.mult,
                     accum_out=scv[:, r, j : j + 1],
                 )
-
-        def mx_pe(b):
-            qt_sb = qtp.tile([P, 8, S], F32, tag="qt")
-            for c in range(8):
-                qt = mxp.tile([P, 512], F32, tag="mx")
-                for g in range(2):
-                    nc.tensor.matmul_mx(
-                        out=qt[:],
-                        lhsT=wc[:, g, P * c : P * (c + 1)].bitcast(FP8X4),
-                        lhsT_scale=ws[:, g, P * c : P * (c + 1)],
-                        rhs=xc[b][:, g, :].bitcast(FP8X4),
-                        rhs_scale=xs[b][:, g, :],
-                        start=(g == 0),
-                        stop=(g == 1),
+                vdone[0] += 1
+                if vdone[0] == W5 * NV:
+                    nc.vector.tensor_tensor(out=scv[:], in0=scv[:], in1=negv[:], op=ALU.add)
+                    yv = small.tile([P, NV, W5], F32)
+                    softmax(scv, NV, yv[:], "v")
+                    nc.sync.dma_start(
+                        out=of[VS : VS + P * NV, :].rearrange("(p r) j -> p (r j)", r=NV),
+                        in_=yv[:].rearrange("p r j -> p (r j)"),
                     )
-                nc.scalar.activation(out=qt_sb[:, c, :], in_=qt[:], func=ACT.Identity, bias=bpp[:, c : c + 1], scale=1.0)
-            qts[b] = qt_sb
 
-        def scores_pe(b):
-            for half in range(2):
+        def mxp_group(b, c):
+            key = "p%d" % b
+            if c == 0:
+                qt_sb = qtp.tile([P, 8, S], F32, tag="qt")
+                qts[b] = qt_sb
+            qt = mxp.tile([P, 512], F32, tag="mx")
+            for g in range(2):
+                nc.tensor.matmul_mx(
+                    out=qt[:],
+                    lhsT=wc[:, g, P * c : P * (c + 1)].bitcast(FP8X4),
+                    lhsT_scale=ws[:, g, P * c : P * (c + 1)],
+                    rhs=xc[key][:, g, :].bitcast(FP8X4),
+                    rhs_scale=xs[key][:, g, :],
+                    start=(g == 0),
+                    stop=(g == 1),
+                )
+            nc.scalar.activation(out=qts[b][:, c, :], in_=qt[:], func=ACT.Identity, bias=bpp[:, c : c + 1], scale=1.0)
+
+        def sc_tile(b, tb):
+            if tb % 2 == 0:
                 sps = sp.tile([P, 2, NWIN], F32, tag="s")
-                for ti in range(2):
-                    tb = 2 * half + ti
-                    lo = KPAD - 2 + P * tb
-                    for c in range(8):
-                        nc.tensor.matmul(
-                            out=sps[:, ti, :],
-                            lhsT=qts[b][:, c, P * tb : P * (tb + 1)],
-                            rhs=kts[b][:, c, lo : lo + NWIN],
-                            start=(c == 0),
-                            stop=(c == 7),
-                        )
-                bm = work.tile([P, 2, NWIN], F32, tag="bm")
-                nc.vector.tensor_tensor(
-                    out=bm[:], in0=sps[:], in1=band[:].unsqueeze(1).to_broadcast([P, 2, NWIN]), op=ALU.mult
-                )
-                slot = 4 * b + 2 * half
-                nc.vector.tensor_reduce(
-                    out=rr[:, slot : slot + 2, 0:MOD],
-                    in_=bm[:].rearrange("p t (m r) -> p t r m", r=MOD),
-                    axis=AX.X,
-                    op=ALU.add,
+                spt[b] = sps
+            lo = KPAD - 2 + P * tb
+            for c in range(8):
+                nc.tensor.matmul(
+                    out=spt[b][:, tb % 2, :],
+                    lhsT=qts[b][:, c, P * tb : P * (tb + 1)],
+                    rhs=kts[b][:, c, lo : lo + NWIN],
+                    start=(c == 0),
+                    stop=(c == 7),
                 )
 
-        def softmax(sc, groups, dest, label):
-            mx = small.tile([P, groups], F32, name="mx" + label)
-            nc.vector.tensor_reduce(out=mx[:], in_=sc[:], axis=AX.X, op=ALU.max)
+        def ex_half(b, half):
+            bm = work.tile([P, 2, NWIN], F32, tag="bm")
             nc.vector.tensor_tensor(
-                out=sc[:], in0=sc[:], in1=mx[:].unsqueeze(2).to_broadcast([P, groups, W5]), op=ALU.subtract
+                out=bm[:], in0=spt[b][:], in1=band[:].unsqueeze(1).to_broadcast([P, 2, NWIN]), op=ALU.mult
             )
-            ex = small.tile([P, groups, W5], F32, name="ex" + label)
-            nc.scalar.activation(out=ex[:], in_=sc[:], func=ACT.Exp, scale=1.0 / 32.0)
-            sm = small.tile([P, groups], F32, name="sm" + label)
-            nc.vector.tensor_reduce(out=sm[:], in_=ex[:], axis=AX.X, op=ALU.add)
-            rs = small.tile([P, groups], F32, name="rs" + label)
-            nc.vector.reciprocal(out=rs[:], in_=sm[:])
-            nc.vector.tensor_tensor(
-                out=dest, in0=ex[:], in1=rs[:].unsqueeze(2).to_broadcast([P, groups, W5]), op=ALU.mult
+            slot = 4 * b + 2 * half
+            nc.vector.tensor_reduce(
+                out=rr[:, slot : slot + 2, 0:MOD],
+                in_=bm[:].rearrange("p t (m r) -> p t r m", r=MOD),
+                axis=AX.X,
+                op=ALU.add,
             )
+            nc.vector.tensor_copy(out=rr[:, slot : slot + 2, MOD : MOD + W5], in_=rr[:, slot : slot + 2, 0:W5])
 
-        stage_w()
-        stage_x(VB, True)
-        stage_x(0, True)
-        stage_k(0, True)
-        qb = rawp.tile([P, 4, D], F32, tag="big")
-        mx_v()
-        mx_pe(0)
-        v_scores(0)
-        stage_x(2, False)
-        stage_k(2, False)
-        scores_pe(0)
-        v_scores(1)
-        mx_pe(2)
-        stage_x(3, False)
-        stage_k(3, False)
-        v_scores(2)
-        scores_pe(2)
-        mx_pe(3)
-        v_scores(3)
-        nc.vector.tensor_tensor(out=scv[:], in0=scv[:], in1=negv[:], op=ALU.add)
-        yv = small.tile([P, 4, W5], F32)
-        softmax(scv, 4, yv[:], "v")
-        nc.sync.dma_start(
-            out=of[S * VB : S * (VB + 1), :].rearrange("(p r) j -> p (r j)", r=4),
-            in_=yv[:].rearrange("p r j -> p (r j)"),
+        alt = ("s", "v")
+        for c in range(4):
+            w_bank(c, alt[c % 2])
+        w_quant(0)
+        for j in range(4):
+            x_bank("v0", j, alt[j % 2])
+        x_quant("v0")
+        load_xp(PE_BATCHES[-1])
+        load_k(PE_BATCHES[-1])
+        for c in range(4, 8):
+            w_bank(c, alt[c % 2])
+        w_quant(1)
+        qb = rawp.tile([P, NV, D], F32, tag="big")
+        for vg in range(1, NV // 4):
+            for j in range(4):
+                x_bank("v%d" % vg, j, alt[j % 2])
+            x_quant("v%d" % vg)
+        first = PE_BATCHES[0]
+        for r in range(4):
+            mxv_group(r, 0)
+        for j in range(4):
+            x_bank("p%d" % first, j, alt[j % 2])
+        x_quant("p%d" % first)
+        for r in range(4):
+            mxv_group(r, 1)
+        for r in range(4, NV):
+            mxv_group(r, 0)
+            mxv_group(r, 1)
+        for tb in range(4):
+            k_bank(first, tb, alt[tb % 2])
+        late_consts()
+        for c in range(8):
+            mxp_group(first, c)
+        vfill(3)
+
+        for gi, b in enumerate(PE_BATCHES):
+            nxt = PE_BATCHES[gi + 1] if gi + 1 < len(PE_BATCHES) else None
+            nkey = "p%d" % nxt if nxt is not None else ""
+            sc_tile(b, 0)
+            if nxt is not None:
+                for j in range(3):
+                    x_bank(nkey, j, "s")
+            vfill(2)
+            sc_tile(b, 1)
+            if nxt is not None:
+                x_bank(nkey, 3, "s")
+                k_bank(nxt, 0, "s")
+                k_bank(nxt, 1, "s")
+                x_quant(nkey)
+            ex_half(b, 0)
+            vfill(2)
+            sc_tile(b, 2)
+            if nxt is not None:
+                k_bank(nxt, 2, "s")
+                k_bank(nxt, 3, "s")
+            sc_tile(b, 3)
+            ex_half(b, 1)
+            if nxt is not None:
+                for c in range(8):
+                    mxp_group(nxt, c)
+                vfill(3)
+
+        sca = small.tile([P, 16, W5], F32)
+        scb = small.tile([P, 16, W5], F32)
+        nc.vector.scalar_tensor_tensor(
+            out=sca[:], in0=rr[:, :, 0:W5], scalar=ind[:, 0:1], in1=negfull[:], op0=ALU.mult, op1=ALU.add
         )
-        scores_pe(3)
-
-        nc.vector.tensor_copy(out=rr[:, :, MOD : MOD + W5], in_=rr[:, :, 0:W5])
-        sc = small.tile([P, 16, W5], F32)
-        nc.vector.tensor_scalar_mul(out=sc[:], in0=rr[:, :, 0:W5], scalar1=ind[:, 0:1])
-        for rho in range(1, MOD):
+        nc.vector.tensor_scalar_mul(out=scb[:], in0=rr[:, :, 1 : 1 + W5], scalar1=ind[:, 1:2])
+        for rho in range(2, MOD):
+            acc = sca if rho % 2 == 0 else scb
             nc.vector.scalar_tensor_tensor(
-                out=sc[:], in0=rr[:, :, rho : rho + W5], scalar=ind[:, rho : rho + 1], in1=sc[:], op0=ALU.mult, op1=ALU.add
+                out=acc[:], in0=rr[:, :, rho : rho + W5], scalar=ind[:, rho : rho + 1], in1=acc[:], op0=ALU.mult, op1=ALU.add
             )
-        scb = sc[:].rearrange("p (b t) j -> p b (t j)", b=4)
-        nc.vector.tensor_tensor(
-            out=scb,
-            in0=scb,
-            in1=neg4[:].rearrange("p t j -> p (t j)").unsqueeze(1).to_broadcast([P, 4, 4 * W5]),
-            op=ALU.add,
-        )
-        softmax(sc, 16, ypad[:, :, 0:16].rearrange("p j t -> p t j"), "p")
+        nc.vector.tensor_tensor(out=sca[:], in0=sca[:], in1=scb[:], op=ALU.add)
+        softmax(sca, 16, ypad[:, :, 0:16].rearrange("p j t -> p t j"), "p")
 
         ta = tp.tile([P, 4, P], F32, tag="tp")
         for j in range(4):
@@ -349,5 +433,6 @@ def tile_crosssliceattention_pa_kernel(tc, x, Wq, bq, k_proj, out):
         nc.vector.tensor_copy(out=z2[:, :, 0:4], in_=ta[:].rearrange("s j p -> s p j"))
         nc.vector.tensor_copy(out=z2[:, :, 4:5], in_=tb4[:, 0:1, :].rearrange("s j p -> s p j"))
         ov = of.rearrange("(t p) j -> t (p j)", p=P)
-        nc.sync.dma_start(out=ov[0:4, :], in_=z2[0:4, :, :].rearrange("s p j -> s (p j)"))
-        nc.sync.dma_start(out=ov[8:16, :], in_=z2[8:16, :, :].rearrange("s p j -> s (p j)"))
+        for b in PE_BATCHES:
+            nc.sync.dma_start(out=ov[4 * b : 4 * b + 4, :], in_=z2[4 * b : 4 * b + 4, :, :].rearrange("s p j -> s (p j)"))
+        vfill(W5 * NV)

@@ -42,8 +42,7 @@ def tile_crosssliceattention_pa_kernel(tc, x, Wq, bq, k_proj, out):
         codes = ctx.enter_context(tc.tile_pool(name="codes", bufs=1))
         work = ctx.enter_context(tc.tile_pool(name="work", bufs=2))
         small = ctx.enter_context(tc.tile_pool(name="small", bufs=1))
-        tp = ctx.enter_context(tc.psum_pool(name="tp", bufs=3))
-        mxp = ctx.enter_context(tc.psum_pool(name="mx", bufs=3))
+        tp = ctx.enter_context(tc.psum_pool(name="banks", bufs=6))
         sp = ctx.enter_context(tc.psum_pool(name="sps", bufs=2))
         ctx.enter_context(tc.manual_schedule())
 
@@ -111,12 +110,15 @@ def tile_crosssliceattention_pa_kernel(tc, x, Wq, bq, k_proj, out):
         nc.gpsimd.memset(band[:], 0.0)
         idw = consts.tile([P, NWIN], F32)
         nc.gpsimd.memset(idw[:], 0.0)
-        neg4 = consts.tile([P, 4, W5], F32)
-        nc.gpsimd.memset(neg4[:], 0.0)
         negv = consts.tile([P, NV, W5], F32)
         nc.gpsimd.memset(negv[:], 0.0)
-        rr = small.tile([P, 16, MOD + W5], F32)
+        rr = small.tile([P, 16, MOD + 1], F32)
         nc.gpsimd.memset(rr[:], 0.0)
+        nc.gpsimd.memset(rr[:, :, MOD : MOD + 1], 1.0)
+        sel = consts.tile([P, 4, W5, MOD + 1], F32)
+        nc.gpsimd.memset(sel[:], 0.0)
+        sc = small.tile([P, 16, W5], F32)
+        nc.gpsimd.memset(sc[:], 0.0)
         ypad = small.tile([P, W5, P], F32)
         nc.gpsimd.memset(ypad[:], 0.0)
 
@@ -141,19 +143,23 @@ def tile_crosssliceattention_pa_kernel(tc, x, Wq, bq, k_proj, out):
             nc.vector.tensor_reduce(
                 out=ind[:], in_=idw[:].rearrange("p (m r) -> p r m", r=MOD), axis=AX.X, op=ALU.add
             )
+            for j in range(W5):
+                nc.vector.tensor_copy(
+                    out=sel[:, :, j, j:MOD], in_=ind[:, 0 : MOD - j].unsqueeze(1).to_broadcast([P, 4, MOD - j])
+                )
+                if j > 0:
+                    nc.vector.tensor_copy(
+                        out=sel[:, :, j, 0:j], in_=ind[:, MOD - j : MOD].unsqueeze(1).to_broadcast([P, 4, j])
+                    )
             for tb, j, p in ((0, 0, 0), (0, 1, 0), (0, 0, 1), (3, 3, 127), (3, 4, 127), (3, 4, 126)):
                 nc.vector.scalar_tensor_tensor(
-                    out=neg4[:, tb, j : j + 1],
+                    out=sel[:, tb, j, MOD : MOD + 1],
                     in0=ident[:, p : p + 1],
                     scalar=-BIG,
-                    in1=neg4[:, tb, j : j + 1],
+                    in1=sel[:, tb, j, MOD : MOD + 1],
                     op0=ALU.mult,
                     op1=ALU.add,
                 )
-            nc.vector.tensor_copy(
-                out=negfull[:].rearrange("p (b t) j -> p b (t j)", b=4),
-                in_=neg4[:].rearrange("p t j -> p (t j)").unsqueeze(1).to_broadcast([P, 4, 4 * W5]),
-            )
             for p in range(P):
                 for r in range(NV):
                     tok = VS + NV * p + r
@@ -169,7 +175,6 @@ def tile_crosssliceattention_pa_kernel(tc, x, Wq, bq, k_proj, out):
                             )
 
         ind = consts.tile([P, MOD], F32)
-        negfull = consts.tile([P, 16, W5], F32)
 
         def evac(eng, out_ap, in_ap):
             if eng == "v":
@@ -243,7 +248,7 @@ def tile_crosssliceattention_pa_kernel(tc, x, Wq, bq, k_proj, out):
         def mxv_group(r, h):
             key = "v%d" % (r // 4)
             cols = slice(P * (r % 4), P * (r % 4 + 1))
-            qv = mxp.tile([P, 512], F32, tag="mx")
+            qv = tp.tile([P, 512], F32, tag="tp")
             for g in range(2):
                 nc.tensor.matmul_mx(
                     out=qv[:],
@@ -307,7 +312,7 @@ def tile_crosssliceattention_pa_kernel(tc, x, Wq, bq, k_proj, out):
             if c == 0:
                 qt_sb = qtp.tile([P, 8, S], F32, tag="qt")
                 qts[b] = qt_sb
-            qt = mxp.tile([P, 512], F32, tag="mx")
+            qt = tp.tile([P, 512], F32, tag="tp")
             for g in range(2):
                 nc.tensor.matmul_mx(
                     out=qt[:],
@@ -346,7 +351,14 @@ def tile_crosssliceattention_pa_kernel(tc, x, Wq, bq, k_proj, out):
                 axis=AX.X,
                 op=ALU.add,
             )
-            nc.vector.tensor_copy(out=rr[:, slot : slot + 2, MOD : MOD + W5], in_=rr[:, slot : slot + 2, 0:W5])
+            pr = work.tile([P, 2, W5, MOD + 1], F32, tag="pr")
+            nc.vector.tensor_tensor(
+                out=pr[:],
+                in0=rr[:, slot : slot + 2, :].unsqueeze(2).to_broadcast([P, 2, W5, MOD + 1]),
+                in1=sel[:, 2 * half : 2 * half + 2, :, :],
+                op=ALU.mult,
+            )
+            nc.vector.tensor_reduce(out=sc[:, slot : slot + 2, :], in_=pr[:], axis=AX.X, op=ALU.add)
 
         alt = ("s", "v")
         for c in range(4):
@@ -371,13 +383,13 @@ def tile_crosssliceattention_pa_kernel(tc, x, Wq, bq, k_proj, out):
         for j in range(4):
             x_bank("p%d" % first, j, alt[j % 2])
         x_quant("p%d" % first)
+        for tb in range(4):
+            k_bank(first, tb, alt[tb % 2])
         for r in range(4):
             mxv_group(r, 1)
         for r in range(4, NV):
             mxv_group(r, 0)
             mxv_group(r, 1)
-        for tb in range(4):
-            k_bank(first, tb, alt[tb % 2])
         late_consts()
         for c in range(8):
             mxp_group(first, c)
@@ -410,19 +422,7 @@ def tile_crosssliceattention_pa_kernel(tc, x, Wq, bq, k_proj, out):
                     mxp_group(nxt, c)
                 vfill(3)
 
-        sca = small.tile([P, 16, W5], F32)
-        scb = small.tile([P, 16, W5], F32)
-        nc.vector.scalar_tensor_tensor(
-            out=sca[:], in0=rr[:, :, 0:W5], scalar=ind[:, 0:1], in1=negfull[:], op0=ALU.mult, op1=ALU.add
-        )
-        nc.vector.tensor_scalar_mul(out=scb[:], in0=rr[:, :, 1 : 1 + W5], scalar1=ind[:, 1:2])
-        for rho in range(2, MOD):
-            acc = sca if rho % 2 == 0 else scb
-            nc.vector.scalar_tensor_tensor(
-                out=acc[:], in0=rr[:, :, rho : rho + W5], scalar=ind[:, rho : rho + 1], in1=acc[:], op0=ALU.mult, op1=ALU.add
-            )
-        nc.vector.tensor_tensor(out=sca[:], in0=sca[:], in1=scb[:], op=ALU.add)
-        softmax(sca, 16, ypad[:, :, 0:16].rearrange("p j t -> p t j"), "p")
+        softmax(sc, 16, ypad[:, :, 0:16].rearrange("p j t -> p t j"), "p")
 
         ta = tp.tile([P, 4, P], F32, tag="tp")
         for j in range(4):

@@ -15,9 +15,11 @@ AX = mybir.AxisListType
 P = 128
 B, S, D = 4, 512, 1024
 W5 = 5
-NV = 4
+NV = 5
 VS = 512
-PE_BATCHES = tuple([b for b in range(B) if not VS <= S * b < VS + P * NV])
+V_GROUPS = [list(range(r, min(r + 4, NV))) for r in range(0, NV, 4)]
+PE_TILES = {b: [t for t in range(4) if not VS <= S * b + P * t < VS + P * NV] for b in range(B)}
+PE_BATCHES = [b for b in range(B) if PE_TILES[b]]
 KPAD = 8
 KW = S + 2 * KPAD
 NWIN = 132
@@ -25,6 +27,16 @@ MOD = 6
 BIG = 1.0e30
 
 FLOPS = 2 * B * S * D * D + 2 * B * S * W5 * D
+
+
+def pieces(n):
+    cuts = []
+    start = 0
+    for size in (4, 2, 1):
+        while n - start >= size:
+            cuts.append((start, size))
+            start += size
+    return cuts
 
 
 def tile_crosssliceattention_pa_kernel(tc, x, Wq, bq, k_proj, out):
@@ -54,51 +66,54 @@ def tile_crosssliceattention_pa_kernel(tc, x, Wq, bq, k_proj, out):
         wv = Wq.rearrange("(u p e) i -> p u e i", p=P, e=2)
         xraw = {}
         kraw = {}
+        ntile = {}
+        groups = ["v%d" % g for g in range(len(V_GROUPS))] + ["p%d" % b for b in PE_BATCHES]
 
         def load_w(u):
             nc.sync.dma_start(out=w_raw[:, u, :, :], in_=wv[:, u, :, :])
 
-        def load_x(key, view):
+        def load_pairs(dst, view, n):
+            for j in range(0, n, 2):
+                hi = min(j + 2, n)
+                nc.sync.dma_start(out=dst[:, j:hi, :], in_=view[:, j:hi, :])
+
+        def load_group(key):
+            idx = int(key[1:])
             xr = rawp.tile([P, 4, D], BF16, tag="xr", bufs=3)
-            for hh in range(2):
-                nc.sync.dma_start(out=xr[:, 2 * hh : 2 * hh + 2, :], in_=view[:, 2 * hh : 2 * hh + 2, :])
             xraw[key] = xr
+            if key[0] == "v":
+                tiles = V_GROUPS[idx]
+                view = xf[VS : VS + P * NV, :].rearrange("(p r) i -> p r i", r=NV)[:, tiles[0] : tiles[-1] + 1, :]
+            else:
+                tiles = PE_TILES[idx]
+                view = xf[S * idx + P * tiles[0] : S * (idx + 1), :].rearrange("(t p) i -> p t i", p=P)
+            ntile[key] = len(tiles)
+            load_pairs(xr, view, len(tiles))
+            if key[0] == "p":
+                kr = rawp.tile([P, 4, D], BF16, name="kraw" + key)
+                kraw[idx] = kr
+                load_pairs(kr, kf[S * idx : S * (idx + 1), :].rearrange("(t p) d -> p t d", p=P), 4)
 
-        def load_xv(vg):
-            view = xf[VS : VS + P * NV, :].rearrange("(p r) i -> p r i", r=NV)
-            load_x("v%d" % vg, view[:, 4 * vg : 4 * vg + 4, :])
+        k_v = rawp.tile([P, NV + 4, D], BF16)
 
-        def load_xp(b):
-            load_x("p%d" % b, xf[S * b : S * (b + 1), :].rearrange("(t p) i -> p t i", p=P))
-
-        def load_k(b):
-            kr = rawp.tile([P, 4, D], BF16, name="kraw%d" % b)
-            view = kf[S * b : S * (b + 1), :].rearrange("(t p) d -> p t d", p=P)
-            for hh in range(2):
-                nc.sync.dma_start(out=kr[:, 2 * hh : 2 * hh + 2, :], in_=view[:, 2 * hh : 2 * hh + 2, :])
-            kraw[b] = kr
+        def load_kv():
+            base = VS - 2
+            nc.sync.dma_start(
+                out=k_v[:, 0:NV, :], in_=kf[base : base + P * NV, :].rearrange("(p c) d -> p c d", c=NV)
+            )
+            nc.sync.dma_start(
+                out=k_v[:, NV : NV + 4, :],
+                in_=kf[base + NV : base + NV + P * NV, :].rearrange("(p c) d -> p c d", c=NV)[:, 0:4, :],
+            )
 
         load_w(0)
         load_w(1)
-        load_xv(0)
+        load_group(groups[0])
         load_w(2)
         load_w(3)
-        for vg in range(1, NV // 4):
-            load_xv(vg)
-        load_xp(PE_BATCHES[0])
-        load_k(PE_BATCHES[0])
-        k_v = rawp.tile([P, NV + 4, D], BF16)
-        base = VS - 2
-        nc.sync.dma_start(
-            out=k_v[:, 0:NV, :], in_=kf[base : base + P * NV, :].rearrange("(p c) d -> p c d", c=NV)
-        )
-        nc.sync.dma_start(
-            out=k_v[:, NV : NV + 4, :],
-            in_=kf[base + NV : base + NV + P * NV, :].rearrange("(p c) d -> p c d", c=NV)[:, 0:4, :],
-        )
-        for b in PE_BATCHES[1:-1]:
-            load_xp(b)
-            load_k(b)
+        load_group(groups[1])
+        load_group(groups[2])
+        load_kv()
 
         ident = consts.tile([P, P], F32)
         make_identity(nc, ident[:])
@@ -219,12 +234,19 @@ def tile_crosssliceattention_pa_kernel(tc, x, Wq, bq, k_proj, out):
             gf = grp[key][:].bitcast(F32).rearrange("p g (c u) -> p g c u", u=2)
             bank = transpose_words(xraw[key][:].bitcast(F32)[:, j, :])
             evac(eng, gf[:, :, P * j : P * (j + 1), :], bank[:].rearrange("p (g u) c -> p g c u", u=2))
+            if j == ntile[key] - 1 and groups.index(key) + 3 < len(groups):
+                load_group(groups[groups.index(key) + 3])
 
         def x_quant(key):
             xcb = codes.tile([P, 2, S], U32, name="xc" + key, align_bytes=64)
             xsb = codes.tile([P, 2, S], U8, name="xs" + key, align_bytes=64)
-            for g in range(2):
-                nc.vector.quantize_mx(out=xcb[:, g, :].bitcast(FP8X4), scales=xsb[:, g, :], in_=grp[key][:, g, :])
+            for t0, tn in pieces(ntile[key]):
+                for g in range(2):
+                    nc.vector.quantize_mx(
+                        out=xcb[:, g, P * t0 : P * (t0 + tn)].bitcast(FP8X4),
+                        scales=xsb[:, g, P * t0 : P * (t0 + tn)],
+                        in_=grp[key][:, g, 4 * P * t0 : 4 * P * (t0 + tn)],
+                    )
             xc[key] = xcb
             xs[key] = xsb
 
@@ -309,83 +331,90 @@ def tile_crosssliceattention_pa_kernel(tc, x, Wq, bq, k_proj, out):
 
         def mxp_group(b, c):
             key = "p%d" % b
+            width = P * ntile[key]
             if c == 0:
                 qt_sb = qtp.tile([P, 8, S], F32, tag="qt")
                 qts[b] = qt_sb
             qt = tp.tile([P, 512], F32, tag="tp")
-            for g in range(2):
-                nc.tensor.matmul_mx(
-                    out=qt[:],
-                    lhsT=wc[:, g, P * c : P * (c + 1)].bitcast(FP8X4),
-                    lhsT_scale=ws[:, g, P * c : P * (c + 1)],
-                    rhs=xc[key][:, g, :].bitcast(FP8X4),
-                    rhs_scale=xs[key][:, g, :],
-                    start=(g == 0),
-                    stop=(g == 1),
-                )
-            nc.scalar.activation(out=qts[b][:, c, :], in_=qt[:], func=ACT.Identity, bias=bpp[:, c : c + 1], scale=1.0)
+            for t0, tn in pieces(ntile[key]):
+                cols = slice(P * t0, P * (t0 + tn))
+                for g in range(2):
+                    nc.tensor.matmul_mx(
+                        out=qt[:, cols],
+                        lhsT=wc[:, g, P * c : P * (c + 1)].bitcast(FP8X4),
+                        lhsT_scale=ws[:, g, P * c : P * (c + 1)],
+                        rhs=xc[key][:, g, cols].bitcast(FP8X4),
+                        rhs_scale=xs[key][:, g, cols],
+                        start=(g == 0),
+                        stop=(g == 1),
+                    )
+            nc.scalar.activation(
+                out=qts[b][:, c, 0:width], in_=qt[:, 0:width], func=ACT.Identity, bias=bpp[:, c : c + 1], scale=1.0
+            )
 
         def sc_tile(b, tb):
-            if tb % 2 == 0:
+            if tb % 2 == 0 or tb == PE_TILES[b][0]:
                 sps = sp.tile([P, 2, NWIN], F32, tag="s")
                 spt[b] = sps
             lo = KPAD - 2 + P * tb
+            col = P * (tb - PE_TILES[b][0])
             for c in range(8):
                 nc.tensor.matmul(
                     out=spt[b][:, tb % 2, :],
-                    lhsT=qts[b][:, c, P * tb : P * (tb + 1)],
+                    lhsT=qts[b][:, c, col : col + P],
                     rhs=kts[b][:, c, lo : lo + NWIN],
                     start=(c == 0),
                     stop=(c == 7),
                 )
 
-        def ex_half(b, half):
+        def ex_half(b, tb):
+            first_tb = max(tb - tb % 2, PE_TILES[b][0])
+            n = tb - first_tb + 1
+            pair = slice(first_tb % 2, first_tb % 2 + n)
+            slots = slice(4 * b + first_tb, 4 * b + tb + 1)
             bm = work.tile([P, 2, NWIN], F32, tag="bm")
             nc.vector.tensor_tensor(
-                out=bm[:], in0=spt[b][:], in1=band[:].unsqueeze(1).to_broadcast([P, 2, NWIN]), op=ALU.mult
+                out=bm[:, 0:n, :], in0=spt[b][:, pair, :], in1=band[:].unsqueeze(1).to_broadcast([P, n, NWIN]), op=ALU.mult
             )
-            slot = 4 * b + 2 * half
             nc.vector.tensor_reduce(
-                out=rr[:, slot : slot + 2, 0:MOD],
-                in_=bm[:].rearrange("p t (m r) -> p t r m", r=MOD),
+                out=rr[:, slots, 0:MOD],
+                in_=bm[:, 0:n, :].rearrange("p t (m r) -> p t r m", r=MOD),
                 axis=AX.X,
                 op=ALU.add,
             )
             pr = work.tile([P, 2, W5, MOD + 1], F32, tag="pr")
             nc.vector.tensor_tensor(
-                out=pr[:],
-                in0=rr[:, slot : slot + 2, :].unsqueeze(2).to_broadcast([P, 2, W5, MOD + 1]),
-                in1=sel[:, 2 * half : 2 * half + 2, :, :],
+                out=pr[:, 0:n, :, :],
+                in0=rr[:, slots, :].unsqueeze(2).to_broadcast([P, n, W5, MOD + 1]),
+                in1=sel[:, first_tb : tb + 1, :, :],
                 op=ALU.mult,
             )
-            nc.vector.tensor_reduce(out=sc[:, slot : slot + 2, :], in_=pr[:], axis=AX.X, op=ALU.add)
+            nc.vector.tensor_reduce(out=sc[:, slots, :], in_=pr[:, 0:n, :, :], axis=AX.X, op=ALU.add)
 
         alt = ("s", "v")
+
+        def x_stage(key):
+            for j in range(ntile[key]):
+                x_bank(key, j, alt[j % 2])
+            x_quant(key)
+
         for c in range(4):
             w_bank(c, alt[c % 2])
         w_quant(0)
-        for j in range(4):
-            x_bank("v0", j, alt[j % 2])
-        x_quant("v0")
-        load_xp(PE_BATCHES[-1])
-        load_k(PE_BATCHES[-1])
+        x_stage("v0")
         for c in range(4, 8):
             w_bank(c, alt[c % 2])
         w_quant(1)
         qb = rawp.tile([P, NV, D], F32, tag="big")
-        for vg in range(1, NV // 4):
-            for j in range(4):
-                x_bank("v%d" % vg, j, alt[j % 2])
-            x_quant("v%d" % vg)
-        first = PE_BATCHES[0]
-        for r in range(4):
+        for r in V_GROUPS[0]:
             mxv_group(r, 0)
-        for j in range(4):
-            x_bank("p%d" % first, j, alt[j % 2])
-        x_quant("p%d" % first)
+        for g in range(1, len(V_GROUPS)):
+            x_stage("v%d" % g)
+        first = PE_BATCHES[0]
+        x_stage("p%d" % first)
         for tb in range(4):
             k_bank(first, tb, alt[tb % 2])
-        for r in range(4):
+        for r in V_GROUPS[0]:
             mxv_group(r, 1)
         for r in range(4, NV):
             mxv_group(r, 0)
@@ -396,31 +425,28 @@ def tile_crosssliceattention_pa_kernel(tc, x, Wq, bq, k_proj, out):
         vfill(3)
 
         for gi, b in enumerate(PE_BATCHES):
-            nxt = PE_BATCHES[gi + 1] if gi + 1 < len(PE_BATCHES) else None
-            nkey = "p%d" % nxt if nxt is not None else ""
-            sc_tile(b, 0)
-            if nxt is not None:
-                for j in range(3):
-                    x_bank(nkey, j, "s")
-            vfill(2)
-            sc_tile(b, 1)
-            if nxt is not None:
-                x_bank(nkey, 3, "s")
-                k_bank(nxt, 0, "s")
-                k_bank(nxt, 1, "s")
-                x_quant(nkey)
-            ex_half(b, 0)
-            vfill(2)
-            sc_tile(b, 2)
-            if nxt is not None:
-                k_bank(nxt, 2, "s")
-                k_bank(nxt, 3, "s")
-            sc_tile(b, 3)
-            ex_half(b, 1)
-            if nxt is not None:
+            jobs = []
+            if gi + 1 < len(PE_BATCHES):
+                nxt = PE_BATCHES[gi + 1]
+                nkey = "p%d" % nxt
+                jobs = [("x", j) for j in range(ntile[nkey])] + [("k", tb) for tb in range(4)]
+            for tb in PE_TILES[b]:
+                sc_tile(b, tb)
+                for kind, j in jobs[0:3]:
+                    if kind == "x":
+                        x_bank(nkey, j, "s")
+                        if j == ntile[nkey] - 1:
+                            x_quant(nkey)
+                    else:
+                        k_bank(nxt, j, "s")
+                jobs = jobs[3:]
+                if tb % 2 == 1:
+                    ex_half(b, tb)
+                vfill(2)
+            if gi + 1 < len(PE_BATCHES):
                 for c in range(8):
                     mxp_group(nxt, c)
-                vfill(3)
+                vfill(1)
 
         softmax(sc, 16, ypad[:, :, 0:16].rearrange("p j t -> p t j"), "p")
 
@@ -434,5 +460,6 @@ def tile_crosssliceattention_pa_kernel(tc, x, Wq, bq, k_proj, out):
         nc.vector.tensor_copy(out=z2[:, :, 4:5], in_=tb4[:, 0:1, :].rearrange("s j p -> s p j"))
         ov = of.rearrange("(t p) j -> t (p j)", p=P)
         for b in PE_BATCHES:
-            nc.sync.dma_start(out=ov[4 * b : 4 * b + 4, :], in_=z2[4 * b : 4 * b + 4, :, :].rearrange("s p j -> s (p j)"))
+            rows = slice(4 * b + PE_TILES[b][0], 4 * b + 4)
+            nc.sync.dma_start(out=ov[rows, :], in_=z2[rows, :, :].rearrange("s p j -> s (p j)"))
         vfill(W5 * NV)

@@ -15,11 +15,9 @@ AX = mybir.AxisListType
 P = 128
 B, S, D = 4, 512, 1024
 W5 = 5
-NV = 5
+NV = 4
 VS = 512
-V_GROUPS = [list(range(r, min(r + 4, NV))) for r in range(0, NV, 4)]
-PE_TILES = {b: [t for t in range(4) if not VS <= S * b + P * t < VS + P * NV] for b in range(B)}
-PE_BATCHES = [b for b in range(B) if PE_TILES[b]]
+PE_BATCHES = tuple([b for b in range(B) if not VS <= S * b < VS + P * NV])
 KPAD = 8
 KW = S + 2 * KPAD
 NWIN = 132
@@ -27,16 +25,6 @@ MOD = 6
 BIG = 1.0e30
 
 FLOPS = 2 * B * S * D * D + 2 * B * S * W5 * D
-
-
-def pieces(n):
-    cuts = []
-    start = 0
-    for size in (4, 2, 1):
-        while n - start >= size:
-            cuts.append((start, size))
-            start += size
-    return cuts
 
 
 def tile_crosssliceattention_pa_kernel(tc, x, Wq, bq, k_proj, out):
@@ -66,54 +54,51 @@ def tile_crosssliceattention_pa_kernel(tc, x, Wq, bq, k_proj, out):
         wv = Wq.rearrange("(u p e) i -> p u e i", p=P, e=2)
         xraw = {}
         kraw = {}
-        ntile = {}
-        groups = ["v%d" % g for g in range(len(V_GROUPS))] + ["p%d" % b for b in PE_BATCHES]
 
         def load_w(u):
             nc.sync.dma_start(out=w_raw[:, u, :, :], in_=wv[:, u, :, :])
 
-        def load_pairs(dst, view, n):
-            for j in range(0, n, 2):
-                hi = min(j + 2, n)
-                nc.sync.dma_start(out=dst[:, j:hi, :], in_=view[:, j:hi, :])
-
-        def load_group(key):
-            idx = int(key[1:])
+        def load_x(key, view):
             xr = rawp.tile([P, 4, D], BF16, tag="xr", bufs=3)
+            for hh in range(2):
+                nc.sync.dma_start(out=xr[:, 2 * hh : 2 * hh + 2, :], in_=view[:, 2 * hh : 2 * hh + 2, :])
             xraw[key] = xr
-            if key[0] == "v":
-                tiles = V_GROUPS[idx]
-                view = xf[VS : VS + P * NV, :].rearrange("(p r) i -> p r i", r=NV)[:, tiles[0] : tiles[-1] + 1, :]
-            else:
-                tiles = PE_TILES[idx]
-                view = xf[S * idx + P * tiles[0] : S * (idx + 1), :].rearrange("(t p) i -> p t i", p=P)
-            ntile[key] = len(tiles)
-            load_pairs(xr, view, len(tiles))
-            if key[0] == "p":
-                kr = rawp.tile([P, 4, D], BF16, name="kraw" + key)
-                kraw[idx] = kr
-                load_pairs(kr, kf[S * idx : S * (idx + 1), :].rearrange("(t p) d -> p t d", p=P), 4)
 
-        k_v = rawp.tile([P, NV + 4, D], BF16)
+        def load_xv(vg):
+            view = xf[VS : VS + P * NV, :].rearrange("(p r) i -> p r i", r=NV)
+            load_x("v%d" % vg, view[:, 4 * vg : 4 * vg + 4, :])
 
-        def load_kv():
-            base = VS - 2
-            nc.sync.dma_start(
-                out=k_v[:, 0:NV, :], in_=kf[base : base + P * NV, :].rearrange("(p c) d -> p c d", c=NV)
-            )
-            nc.sync.dma_start(
-                out=k_v[:, NV : NV + 4, :],
-                in_=kf[base + NV : base + NV + P * NV, :].rearrange("(p c) d -> p c d", c=NV)[:, 0:4, :],
-            )
+        def load_xp(b):
+            load_x("p%d" % b, xf[S * b : S * (b + 1), :].rearrange("(t p) i -> p t i", p=P))
+
+        def load_k(b):
+            kr = rawp.tile([P, 4, D], BF16, name="kraw%d" % b)
+            view = kf[S * b : S * (b + 1), :].rearrange("(t p) d -> p t d", p=P)
+            for hh in range(2):
+                nc.sync.dma_start(out=kr[:, 2 * hh : 2 * hh + 2, :], in_=view[:, 2 * hh : 2 * hh + 2, :])
+            kraw[b] = kr
 
         load_w(0)
         load_w(1)
-        load_group(groups[0])
+        load_xv(0)
         load_w(2)
         load_w(3)
-        load_group(groups[1])
-        load_group(groups[2])
-        load_kv()
+        for vg in range(1, NV // 4):
+            load_xv(vg)
+        load_xp(PE_BATCHES[0])
+        load_k(PE_BATCHES[0])
+        k_v = rawp.tile([P, NV + 4, D], BF16)
+        base = VS - 2
+        nc.sync.dma_start(
+            out=k_v[:, 0:NV, :], in_=kf[base : base + P * NV, :].rearrange("(p c) d -> p c d", c=NV)
+        )
+        nc.sync.dma_start(
+            out=k_v[:, NV : NV + 4, :],
+            in_=kf[base + NV : base + NV + P * NV, :].rearrange("(p c) d -> p c d", c=NV)[:, 0:4, :],
+        )
+        for b in PE_BATCHES[1:-1]:
+            load_xp(b)
+            load_k(b)
 
         ident = consts.tile([P, P], F32)
         make_identity(nc, ident[:])
@@ -121,21 +106,6 @@ def tile_crosssliceattention_pa_kernel(tc, x, Wq, bq, k_proj, out):
         nc.gpsimd.memset(warm[:], 0.0)
         warm2 = consts.tile([P, 1], F32)
         nc.scalar.activation(out=warm2[:], in_=warm[:], func=ACT.Exp)
-        band = consts.tile([P, NWIN], F32)
-        nc.gpsimd.memset(band[:], 0.0)
-        idw = consts.tile([P, NWIN], F32)
-        nc.gpsimd.memset(idw[:], 0.0)
-        negv = consts.tile([P, NV, W5], F32)
-        nc.gpsimd.memset(negv[:], 0.0)
-        rr = small.tile([P, 16, MOD + 1], F32)
-        nc.gpsimd.memset(rr[:], 0.0)
-        nc.gpsimd.memset(rr[:, :, MOD : MOD + 1], 1.0)
-        sel = consts.tile([P, 4, W5, MOD + 1], F32)
-        nc.gpsimd.memset(sel[:], 0.0)
-        sc = small.tile([P, 16, W5], F32)
-        nc.gpsimd.memset(sc[:], 0.0)
-        ypad = small.tile([P, W5, P], F32)
-        nc.gpsimd.memset(ypad[:], 0.0)
 
         bt = tp.tile([P, 4, P], F32, tag="tp")
         nc.tensor.transpose(bt[:, 0, :], brow[:].bitcast(F32), ident[:])
@@ -151,45 +121,47 @@ def tile_crosssliceattention_pa_kernel(tc, x, Wq, bq, k_proj, out):
         bpp = consts.tile([P, 8], F32)
         nc.vector.tensor_copy(out=bpp[:], in_=bw[:].bitcast(BF16))
 
-        def late_consts():
-            for j in range(W5):
-                nc.vector.tensor_tensor(out=band[:, j : j + P], in0=band[:, j : j + P], in1=ident[:], op=ALU.add)
-            nc.vector.tensor_copy(out=idw[:, 0:P], in_=ident[:])
-            nc.vector.tensor_reduce(
-                out=ind[:], in_=idw[:].rearrange("p (m r) -> p r m", r=MOD), axis=AX.X, op=ALU.add
-            )
-            for j in range(W5):
-                nc.vector.tensor_copy(
-                    out=sel[:, :, j, j:MOD], in_=ind[:, 0 : MOD - j].unsqueeze(1).to_broadcast([P, 4, MOD - j])
-                )
-                if j > 0:
-                    nc.vector.tensor_copy(
-                        out=sel[:, :, j, 0:j], in_=ind[:, MOD - j : MOD].unsqueeze(1).to_broadcast([P, 4, j])
-                    )
-            for tb, j, p in ((0, 0, 0), (0, 1, 0), (0, 0, 1), (3, 3, 127), (3, 4, 127), (3, 4, 126)):
-                nc.vector.scalar_tensor_tensor(
-                    out=sel[:, tb, j, MOD : MOD + 1],
-                    in0=ident[:, p : p + 1],
-                    scalar=-BIG,
-                    in1=sel[:, tb, j, MOD : MOD + 1],
-                    op0=ALU.mult,
-                    op1=ALU.add,
-                )
-            for p in range(P):
-                for r in range(NV):
-                    tok = VS + NV * p + r
-                    for j in range(W5):
-                        if (tok + j - 2) // S != tok // S:
-                            nc.vector.scalar_tensor_tensor(
-                                out=negv[:, r, j : j + 1],
-                                in0=ident[:, p : p + 1],
-                                scalar=-BIG,
-                                in1=negv[:, r, j : j + 1],
-                                op0=ALU.mult,
-                                op1=ALU.add,
-                            )
-
+        band = consts.tile([P, NWIN], F32)
+        nc.gpsimd.memset(band[:], 0.0)
+        for j in range(W5):
+            nc.gpsimd.tensor_tensor(out=band[:, j : j + P], in0=band[:, j : j + P], in1=ident[:], op=ALU.add)
+        idw = consts.tile([P, NWIN], F32)
+        nc.gpsimd.memset(idw[:], 0.0)
+        nc.gpsimd.tensor_copy(out=idw[:, 0:P], in_=ident[:])
         ind = consts.tile([P, MOD], F32)
+        nc.vector.tensor_reduce(out=ind[:], in_=idw[:].rearrange("p (m r) -> p r m", r=MOD), axis=AX.X, op=ALU.add)
+        sel = consts.tile([P, 4, W5, MOD + 1], F32)
+        nc.gpsimd.memset(sel[:], 0.0)
+        for j in range(W5):
+            nc.gpsimd.tensor_copy(
+                out=sel[:, :, j, j:MOD], in_=ind[:, 0 : MOD - j].unsqueeze(1).to_broadcast([P, 4, MOD - j])
+            )
+            if j > 0:
+                nc.gpsimd.tensor_copy(
+                    out=sel[:, :, j, 0:j], in_=ind[:, MOD - j : MOD].unsqueeze(1).to_broadcast([P, 4, j])
+                )
+        for tb, j, c in ((0, 0, 1), (0, 1, 0), (3, 3, NWIN - 1), (3, 4, NWIN - 2)):
+            nc.gpsimd.tensor_scalar(
+                out=sel[:, tb, j, MOD : MOD + 1], in0=band[:, c : c + 1], scalar1=-BIG, scalar2=0.0, op0=ALU.mult, op1=ALU.add
+            )
+        negv = consts.tile([P, NV, W5], F32)
+        nc.gpsimd.memset(negv[:], 0.0)
+        for r, j0, j1, p in ((0, 0, 2, 0), (1, 0, 1, 0), (2, 4, 5, P - 1), (3, 3, 5, P - 1)):
+            nc.gpsimd.tensor_scalar(
+                out=negv[:, r, j0:j1],
+                in0=ident[:, p : p + 1].to_broadcast([P, j1 - j0]),
+                scalar1=-BIG,
+                scalar2=0.0,
+                op0=ALU.mult,
+                op1=ALU.add,
+            )
+        rr = small.tile([P, 16, MOD + 1], F32)
+        nc.gpsimd.memset(rr[:], 0.0)
+        nc.gpsimd.memset(rr[:, :, MOD : MOD + 1], 1.0)
+        sc = small.tile([P, 16, W5], F32)
+        nc.gpsimd.memset(sc[:], 0.0)
+        ypad = small.tile([P, W5, P], F32)
+        nc.gpsimd.memset(ypad[:], 0.0)
 
         def evac(eng, out_ap, in_ap):
             if eng == "v":
@@ -234,19 +206,12 @@ def tile_crosssliceattention_pa_kernel(tc, x, Wq, bq, k_proj, out):
             gf = grp[key][:].bitcast(F32).rearrange("p g (c u) -> p g c u", u=2)
             bank = transpose_words(xraw[key][:].bitcast(F32)[:, j, :])
             evac(eng, gf[:, :, P * j : P * (j + 1), :], bank[:].rearrange("p (g u) c -> p g c u", u=2))
-            if j == ntile[key] - 1 and groups.index(key) + 3 < len(groups):
-                load_group(groups[groups.index(key) + 3])
 
         def x_quant(key):
             xcb = codes.tile([P, 2, S], U32, name="xc" + key, align_bytes=64)
             xsb = codes.tile([P, 2, S], U8, name="xs" + key, align_bytes=64)
-            for t0, tn in pieces(ntile[key]):
-                for g in range(2):
-                    nc.vector.quantize_mx(
-                        out=xcb[:, g, P * t0 : P * (t0 + tn)].bitcast(FP8X4),
-                        scales=xsb[:, g, P * t0 : P * (t0 + tn)],
-                        in_=grp[key][:, g, 4 * P * t0 : 4 * P * (t0 + tn)],
-                    )
+            for g in range(2):
+                nc.vector.quantize_mx(out=xcb[:, g, :].bitcast(FP8X4), scales=xsb[:, g, :], in_=grp[key][:, g, :])
             xc[key] = xcb
             xs[key] = xsb
 
@@ -331,122 +296,116 @@ def tile_crosssliceattention_pa_kernel(tc, x, Wq, bq, k_proj, out):
 
         def mxp_group(b, c):
             key = "p%d" % b
-            width = P * ntile[key]
             if c == 0:
                 qt_sb = qtp.tile([P, 8, S], F32, tag="qt")
                 qts[b] = qt_sb
             qt = tp.tile([P, 512], F32, tag="tp")
-            for t0, tn in pieces(ntile[key]):
-                cols = slice(P * t0, P * (t0 + tn))
-                for g in range(2):
-                    nc.tensor.matmul_mx(
-                        out=qt[:, cols],
-                        lhsT=wc[:, g, P * c : P * (c + 1)].bitcast(FP8X4),
-                        lhsT_scale=ws[:, g, P * c : P * (c + 1)],
-                        rhs=xc[key][:, g, cols].bitcast(FP8X4),
-                        rhs_scale=xs[key][:, g, cols],
-                        start=(g == 0),
-                        stop=(g == 1),
-                    )
-            nc.scalar.activation(
-                out=qts[b][:, c, 0:width], in_=qt[:, 0:width], func=ACT.Identity, bias=bpp[:, c : c + 1], scale=1.0
-            )
+            for g in range(2):
+                nc.tensor.matmul_mx(
+                    out=qt[:],
+                    lhsT=wc[:, g, P * c : P * (c + 1)].bitcast(FP8X4),
+                    lhsT_scale=ws[:, g, P * c : P * (c + 1)],
+                    rhs=xc[key][:, g, :].bitcast(FP8X4),
+                    rhs_scale=xs[key][:, g, :],
+                    start=(g == 0),
+                    stop=(g == 1),
+                )
+            nc.scalar.activation(out=qts[b][:, c, :], in_=qt[:], func=ACT.Identity, bias=bpp[:, c : c + 1], scale=1.0)
 
         def sc_tile(b, tb):
-            if tb % 2 == 0 or tb == PE_TILES[b][0]:
+            if tb % 2 == 0:
                 sps = sp.tile([P, 2, NWIN], F32, tag="s")
                 spt[b] = sps
             lo = KPAD - 2 + P * tb
-            col = P * (tb - PE_TILES[b][0])
             for c in range(8):
                 nc.tensor.matmul(
                     out=spt[b][:, tb % 2, :],
-                    lhsT=qts[b][:, c, col : col + P],
+                    lhsT=qts[b][:, c, P * tb : P * (tb + 1)],
                     rhs=kts[b][:, c, lo : lo + NWIN],
                     start=(c == 0),
                     stop=(c == 7),
                 )
 
-        def ex_half(b, tb):
-            first_tb = max(tb - tb % 2, PE_TILES[b][0])
-            n = tb - first_tb + 1
-            pair = slice(first_tb % 2, first_tb % 2 + n)
-            slots = slice(4 * b + first_tb, 4 * b + tb + 1)
+        def ex_half(b, half):
             bm = work.tile([P, 2, NWIN], F32, tag="bm")
             nc.vector.tensor_tensor(
-                out=bm[:, 0:n, :], in0=spt[b][:, pair, :], in1=band[:].unsqueeze(1).to_broadcast([P, n, NWIN]), op=ALU.mult
+                out=bm[:], in0=spt[b][:], in1=band[:].unsqueeze(1).to_broadcast([P, 2, NWIN]), op=ALU.mult
             )
+            slot = 4 * b + 2 * half
             nc.vector.tensor_reduce(
-                out=rr[:, slots, 0:MOD],
-                in_=bm[:, 0:n, :].rearrange("p t (m r) -> p t r m", r=MOD),
+                out=rr[:, slot : slot + 2, 0:MOD],
+                in_=bm[:].rearrange("p t (m r) -> p t r m", r=MOD),
                 axis=AX.X,
                 op=ALU.add,
             )
             pr = work.tile([P, 2, W5, MOD + 1], F32, tag="pr")
             nc.vector.tensor_tensor(
-                out=pr[:, 0:n, :, :],
-                in0=rr[:, slots, :].unsqueeze(2).to_broadcast([P, n, W5, MOD + 1]),
-                in1=sel[:, first_tb : tb + 1, :, :],
+                out=pr[:],
+                in0=rr[:, slot : slot + 2, :].unsqueeze(2).to_broadcast([P, 2, W5, MOD + 1]),
+                in1=sel[:, 2 * half : 2 * half + 2, :, :],
                 op=ALU.mult,
             )
-            nc.vector.tensor_reduce(out=sc[:, slots, :], in_=pr[:, 0:n, :, :], axis=AX.X, op=ALU.add)
-
-        alt = ("s", "v")
-
-        def x_stage(key):
-            for j in range(ntile[key]):
-                x_bank(key, j, alt[j % 2])
-            x_quant(key)
+            nc.vector.tensor_reduce(out=sc[:, slot : slot + 2, :], in_=pr[:], axis=AX.X, op=ALU.add)
 
         for c in range(4):
-            w_bank(c, alt[c % 2])
+            w_bank(c, "s")
         w_quant(0)
-        x_stage("v0")
+        for j in range(4):
+            x_bank("v0", j, "s")
+        x_quant("v0")
+        load_xp(PE_BATCHES[-1])
+        load_k(PE_BATCHES[-1])
         for c in range(4, 8):
-            w_bank(c, alt[c % 2])
+            w_bank(c, "s")
         w_quant(1)
         qb = rawp.tile([P, NV, D], F32, tag="big")
-        for r in V_GROUPS[0]:
-            mxv_group(r, 0)
-        for g in range(1, len(V_GROUPS)):
-            x_stage("v%d" % g)
+        for vg in range(1, NV // 4):
+            for j in range(4):
+                x_bank("v%d" % vg, j, "s")
+            x_quant("v%d" % vg)
         first = PE_BATCHES[0]
-        x_stage("p%d" % first)
+        for r in range(4):
+            mxv_group(r, 0)
+        for j in range(4):
+            x_bank("p%d" % first, j, "s")
+        x_quant("p%d" % first)
         for tb in range(4):
-            k_bank(first, tb, alt[tb % 2])
-        for r in V_GROUPS[0]:
+            k_bank(first, tb, "s")
+        for r in range(4):
             mxv_group(r, 1)
         for r in range(4, NV):
             mxv_group(r, 0)
             mxv_group(r, 1)
-        late_consts()
         for c in range(8):
             mxp_group(first, c)
         vfill(3)
 
         for gi, b in enumerate(PE_BATCHES):
-            jobs = []
-            if gi + 1 < len(PE_BATCHES):
-                nxt = PE_BATCHES[gi + 1]
-                nkey = "p%d" % nxt
-                jobs = [("x", j) for j in range(ntile[nkey])] + [("k", tb) for tb in range(4)]
-            for tb in PE_TILES[b]:
-                sc_tile(b, tb)
-                for kind, j in jobs[0:3]:
-                    if kind == "x":
-                        x_bank(nkey, j, "s")
-                        if j == ntile[nkey] - 1:
-                            x_quant(nkey)
-                    else:
-                        k_bank(nxt, j, "s")
-                jobs = jobs[3:]
-                if tb % 2 == 1:
-                    ex_half(b, tb)
-                vfill(2)
-            if gi + 1 < len(PE_BATCHES):
+            nxt = PE_BATCHES[gi + 1] if gi + 1 < len(PE_BATCHES) else None
+            nkey = "p%d" % nxt if nxt is not None else ""
+            sc_tile(b, 0)
+            if nxt is not None:
+                for j in range(3):
+                    x_bank(nkey, j, "s")
+            vfill(2)
+            sc_tile(b, 1)
+            if nxt is not None:
+                x_bank(nkey, 3, "s")
+                k_bank(nxt, 0, "s")
+                k_bank(nxt, 1, "s")
+                x_quant(nkey)
+            ex_half(b, 0)
+            vfill(2)
+            sc_tile(b, 2)
+            if nxt is not None:
+                k_bank(nxt, 2, "s")
+                k_bank(nxt, 3, "s")
+            sc_tile(b, 3)
+            ex_half(b, 1)
+            if nxt is not None:
                 for c in range(8):
                     mxp_group(nxt, c)
-                vfill(1)
+                vfill(3)
 
         softmax(sc, 16, ypad[:, :, 0:16].rearrange("p j t -> p t j"), "p")
 
@@ -460,6 +419,5 @@ def tile_crosssliceattention_pa_kernel(tc, x, Wq, bq, k_proj, out):
         nc.vector.tensor_copy(out=z2[:, :, 4:5], in_=tb4[:, 0:1, :].rearrange("s j p -> s p j"))
         ov = of.rearrange("(t p) j -> t (p j)", p=P)
         for b in PE_BATCHES:
-            rows = slice(4 * b + PE_TILES[b][0], 4 * b + 4)
-            nc.sync.dma_start(out=ov[rows, :], in_=z2[rows, :, :].rearrange("s p j -> s (p j)"))
+            nc.sync.dma_start(out=ov[4 * b : 4 * b + 4, :], in_=z2[4 * b : 4 * b + 4, :, :].rearrange("s p j -> s (p j)"))
         vfill(W5 * NV)

@@ -274,7 +274,7 @@ def tile_crosssliceattention_pa_kernel(tc, x, Wq, bq, k_proj, out):
                 if vdone[0] >= W5 * NV:
                     return
                 r, j = divmod(vdone[0], W5)
-                junk = work.tile([P, D], F32, tag="junk", bufs=1)
+                junk = work.tile([P, D], F32, tag="junk", bufs=3)
                 nc.vector.scalar_tensor_tensor(
                     out=junk[:],
                     in0=qb[:, r, :],

from contextlib import ExitStack

import concourse.mybir as mybir
from concourse.masks import make_identity

F32 = mybir.dt.float32
BF16 = mybir.dt.bfloat16
U32 = mybir.dt.uint32
U8 = mybir.dt.uint8
FP8X4 = mybir.dt.float8_e4m3fn_x4
ALU = mybir.AluOpType
ACT = mybir.ActivationFunctionType
AX = mybir.AxisListType

P = 128
B, S, D = 4, 512, 1024
W5 = 5
NV = 4
VS = 512
PE_BATCHES = tuple([b for b in range(B) if not VS <= S * b < VS + P * NV])
KPAD = 8
KW = S + 2 * KPAD
NWIN = 132
MOD = 6
BIG = 1.0e30

FLOPS = 2 * B * S * D * D + 2 * B * S * W5 * D


def tile_crosssliceattention_pa_kernel(tc, x, Wq, bq, k_proj, out):
    nc = tc.nc
    xf = x.flatten_outer_dims()
    kf = k_proj.flatten_outer_dims()
    of = out.flatten_outer_dims()

    with ExitStack() as ctx:
        consts = ctx.enter_context(tc.tile_pool(name="consts", bufs=1))
        rawp = ctx.enter_context(tc.tile_pool(name="raw", bufs=1))
        gp = ctx.enter_context(tc.tile_pool(name="grouped", bufs=2))
        ktp = ctx.enter_context(tc.tile_pool(name="kt", bufs=2))
        qtp = ctx.enter_context(tc.tile_pool(name="qt", bufs=2))
        codes = ctx.enter_context(tc.tile_pool(name="codes", bufs=1))
        work = ctx.enter_context(tc.tile_pool(name="work", bufs=2))
        small = ctx.enter_context(tc.tile_pool(name="small", bufs=1))
        tp = ctx.enter_context(tc.psum_pool(name="banks", bufs=6))
        sp = ctx.enter_context(tc.psum_pool(name="sps", bufs=2))
        ctx.enter_context(tc.manual_schedule())

        brow = consts.tile([P, 2 * P], BF16)
        nc.vector.memset(brow[:], 0.0)
        nc.sync.dma_start(out=brow[0:4, :], in_=bq.rearrange("(u w) -> u w", u=4))

        w_raw = rawp.tile([P, 4, 2, D], BF16, tag="big")
        wv = Wq.rearrange("(u p e) i -> p u e i", p=P, e=2)
        xraw = {}
        kraw = {}

        def load_w(u):
            nc.sync.dma_start(out=w_raw[:, u, :, :], in_=wv[:, u, :, :])

        def load_x(key, view):
            xr = rawp.tile([P, 4, D], BF16, tag="xr", bufs=3)
            for hh in range(2):
                nc.sync.dma_start(out=xr[:, 2 * hh : 2 * hh + 2, :], in_=view[:, 2 * hh : 2 * hh + 2, :])
            xraw[key] = xr

        def load_xv(vg):
            view = xf[VS : VS + P * NV, :].rearrange("(p r) i -> p r i", r=NV)
            load_x("v%d" % vg, view[:, 4 * vg : 4 * vg + 4, :])

        def load_xp(b):
            load_x("p%d" % b, xf[S * b : S * (b + 1), :].rearrange("(t p) i -> p t i", p=P))

        def load_k(b):
            kr = rawp.tile([P, 4, D], BF16, name="kraw%d" % b)
            view = kf[S * b : S * (b + 1), :].rearrange("(t p) d -> p t d", p=P)
            for hh in range(2):
                nc.sync.dma_start(out=kr[:, 2 * hh : 2 * hh + 2, :], in_=view[:, 2 * hh : 2 * hh + 2, :])
            kraw[b] = kr

        load_w(0)
        load_w(1)
        load_xv(0)
        load_w(2)
        load_w(3)
        for vg in range(1, NV // 4):
            load_xv(vg)
        load_xp(PE_BATCHES[0])
        load_k(PE_BATCHES[0])
        k_v = rawp.tile([P, NV + 4, D], BF16)
        base = VS - 2
        nc.sync.dma_start(
            out=k_v[:, 0:NV, :], in_=kf[base : base + P * NV, :].rearrange("(p c) d -> p c d", c=NV)
        )
        nc.sync.dma_start(
            out=k_v[:, NV : NV + 4, :],
            in_=kf[base + NV : base + NV + P * NV, :].rearrange("(p c) d -> p c d", c=NV)[:, 0:4, :],
        )
        for b in PE_BATCHES[1:-1]:
            load_xp(b)
            load_k(b)

        ident = consts.tile([P, P], F32)
        make_identity(nc, ident[:])
        warm = consts.tile([P, 1], F32)
        nc.gpsimd.memset(warm[:], 0.0)
        warm2 = consts.tile([P, 1], F32)
        nc.scalar.activation(out=warm2[:], in_=warm[:], func=ACT.Exp)

        bt = tp.tile([P, 4, P], F32, tag="tp")
        nc.tensor.transpose(bt[:, 0, :], brow[:].bitcast(F32), ident[:])
        bw = consts.tile([P, 4], F32)
        nc.vector.tensor_copy(out=bw[:], in_=bt[:, 0, 0:4])
        rep = consts.tile([P, 4, P], F32)
        nc.vector.tensor_copy(out=rep[:], in_=bw[:].unsqueeze(2).to_broadcast([P, 4, P]))
        bbank = tp.tile([P, 4, P], F32, tag="tp")
        for u in range(4):
            nc.tensor.transpose(bbank[:, u, :], rep[:, u, :], ident[:])
        bb = consts.tile([P, D], BF16)
        nc.vector.tensor_copy(out=bb[:].bitcast(F32), in_=bbank[:].rearrange("p u w -> p (u w)"))
        bpp = consts.tile([P, 8], F32)
        nc.vector.tensor_copy(out=bpp[:], in_=bw[:].bitcast(BF16))

        band = consts.tile([P, NWIN], F32)
        nc.gpsimd.memset(band[:], 0.0)
        for j in range(W5):
            nc.gpsimd.tensor_tensor(out=band[:, j : j + P], in0=band[:, j : j + P], in1=ident[:], op=ALU.add)
        idw = consts.tile([P, NWIN], F32)
        nc.gpsimd.memset(idw[:], 0.0)
        nc.gpsimd.tensor_copy(out=idw[:, 0:P], in_=ident[:])
        ind = consts.tile([P, MOD], F32)
        nc.vector.tensor_reduce(out=ind[:], in_=idw[:].rearrange("p (m r) -> p r m", r=MOD), axis=AX.X, op=ALU.add)
        sel = consts.tile([P, 4, W5, MOD + 1], F32)
        nc.gpsimd.memset(sel[:], 0.0)
        for j in range(W5):
            nc.gpsimd.tensor_copy(
                out=sel[:, :, j, j:MOD], in_=ind[:, 0 : MOD - j].unsqueeze(1).to_broadcast([P, 4, MOD - j])
            )
            if j > 0:
                nc.gpsimd.tensor_copy(
                    out=sel[:, :, j, 0:j], in_=ind[:, MOD - j : MOD].unsqueeze(1).to_broadcast([P, 4, j])
                )
        for tb, j, c in ((0, 0, 1), (0, 1, 0), (3, 3, NWIN - 1), (3, 4, NWIN - 2)):
            nc.gpsimd.tensor_scalar(
                out=sel[:, tb, j, MOD : MOD + 1], in0=band[:, c : c + 1], scalar1=-BIG, scalar2=0.0, op0=ALU.mult, op1=ALU.add
            )
        negv = consts.tile([P, NV, W5], F32)
        nc.gpsimd.memset(negv[:], 0.0)
        for r, j0, j1, p in ((0, 0, 2, 0), (1, 0, 1, 0), (2, 4, 5, P - 1), (3, 3, 5, P - 1)):
            nc.gpsimd.tensor_scalar(
                out=negv[:, r, j0:j1],
                in0=ident[:, p : p + 1].to_broadcast([P, j1 - j0]),
                scalar1=-BIG,
                scalar2=0.0,
                op0=ALU.mult,
                op1=ALU.add,
            )
        rr = small.tile([P, 16, MOD + 1], F32)
        nc.gpsimd.memset(rr[:], 0.0)
        nc.gpsimd.memset(rr[:, :, MOD : MOD + 1], 1.0)
        sc = small.tile([P, 16, W5], F32)
        nc.gpsimd.memset(sc[:], 0.0)
        ypad = small.tile([P, W5, P], F32)
        nc.gpsimd.memset(ypad[:], 0.0)

        def evac(eng, out_ap, in_ap):
            if eng == "v":
                nc.vector.tensor_copy(out=out_ap, in_=in_ap)
            else:
                nc.scalar.copy(out=out_ap, in_=in_ap)

        def transpose_words(words):
            bank = tp.tile([P, 4, P], F32, tag="tp")
            for blk in range(4):
                nc.tensor.transpose(bank[:, blk, :], words[:, P * blk : P * (blk + 1)], ident[:])
            return bank

        wc = codes.tile([P, 2, D], U32, align_bytes=64)
        ws = codes.tile([P, 2, D], U8, align_bytes=64)
        gw = ktp.tile([P, 2, 4 * D], BF16, tag="kt", align_bytes=64)
        gwf = gw[:].bitcast(F32).rearrange("p g (c u) -> p g c u", u=2)
        ww = w_raw[:].bitcast(F32)
        xc = {}
        xs = {}
        grp = {}
        kts = {}
        qts = {}
        spt = {}

        def w_bank(c, eng):
            bank = transpose_words(ww[:, c // 2, c % 2, :])
            evac(eng, gwf[:, :, P * c : P * (c + 1), :], bank[:].rearrange("p (g u) c -> p g c u", u=2))

        def w_quant(h):
            for g in range(2):
                nc.vector.quantize_mx(
                    out=wc[:, g, 512 * h : 512 * (h + 1)].bitcast(FP8X4),
                    scales=ws[:, g, 512 * h : 512 * (h + 1)],
                    in_=gw[:, g, 2048 * h : 2048 * (h + 1)],
                )

        def x_bank(key, j, eng):
            if j == 0:
                gt = gp.tile([P, 2, 4 * S], BF16, tag="g", align_bytes=64)
                grp[key] = gt
            gf = grp[key][:].bitcast(F32).rearrange("p g (c u) -> p g c u", u=2)
            bank = transpose_words(xraw[key][:].bitcast(F32)[:, j, :])
            evac(eng, gf[:, :, P * j : P * (j + 1), :], bank[:].rearrange("p (g u) c -> p g c u", u=2))

        def x_quant(key):
            xcb = codes.tile([P, 2, S], U32, name="xc" + key, align_bytes=64)
            xsb = codes.tile([P, 2, S], U8, name="xs" + key, align_bytes=64)
            for g in range(2):
                nc.vector.quantize_mx(out=xcb[:, g, :].bitcast(FP8X4), scales=xsb[:, g, :], in_=grp[key][:, g, :])
            xc[key] = xcb
            xs[key] = xsb

        def k_bank(b, tb, eng):
            if tb == 0:
                kt = ktp.tile([P, 8, KW], F32, tag="kt", align_bytes=64)
                nc.gpsimd.memset(kt[:, :, 0:KPAD], 0.0)
                nc.gpsimd.memset(kt[:, :, KPAD + S : KW], 0.0)
                kts[b] = kt
            bank = transpose_words(kraw[b][:].bitcast(F32)[:, tb, :])
            lo = KPAD + P * tb
            evac(
                eng,
                kts[b][:, :, lo : lo + P].rearrange("p (u e) k -> p u e k", e=2),
                bank[:].bitcast(BF16).rearrange("p u (k e) -> p u e k", e=2),
            )

        scv = small.tile([P, NV, W5], F32)
        vdone = [0]

        def mxv_group(r, h):
            key = "v%d" % (r // 4)
            cols = slice(P * (r % 4), P * (r % 4 + 1))
            qv = tp.tile([P, 512], F32, tag="tp")
            for g in range(2):
                nc.tensor.matmul_mx(
                    out=qv[:],
                    lhsT=xc[key][:, g, cols].bitcast(FP8X4),
                    lhsT_scale=xs[key][:, g, cols],
                    rhs=wc[:, g, 512 * h : 512 * (h + 1)].bitcast(FP8X4),
                    rhs_scale=ws[:, g, 512 * h : 512 * (h + 1)],
                    start=(g == 0),
                    stop=(g == 1),
                )
            nc.vector.tensor_tensor(
                out=qb[:, r, 512 * h : 512 * (h + 1)].rearrange("p (u q e) -> p u q e", u=2, e=2),
                in0=qv[:].rearrange("p (u e q) -> p u q e", u=2, e=2),
                in1=bb[:, 512 * h : 512 * (h + 1)].rearrange("p (u q e) -> p u q e", u=2, e=2),
                op=ALU.add,
            )

        def softmax(sc_t, groups, dest, label):
            mx = small.tile([P, groups], F32, name="mx" + label)
            nc.vector.tensor_reduce(out=mx[:], in_=sc_t[:], axis=AX.X, op=ALU.max)
            nc.vector.tensor_tensor(
                out=sc_t[:], in0=sc_t[:], in1=mx[:].unsqueeze(2).to_broadcast([P, groups, W5]), op=ALU.subtract
            )
            ex = small.tile([P, groups, W5], F32, name="ex" + label)
            nc.scalar.activation(out=ex[:], in_=sc_t[:], func=ACT.Exp, scale=1.0 / 32.0)
            sm = small.tile([P, groups], F32, name="sm" + label)
            nc.vector.tensor_reduce(out=sm[:], in_=ex[:], axis=AX.X, op=ALU.add)
            rs = small.tile([P, groups], F32, name="rs" + label)
            nc.vector.reciprocal(out=rs[:], in_=sm[:])
            nc.vector.tensor_tensor(
                out=dest, in0=ex[:], in1=rs[:].unsqueeze(2).to_broadcast([P, groups, W5]), op=ALU.mult
            )

        def vfill(n):
            for i in range(n):
                if vdone[0] >= W5 * NV:
                    return
                r, j = divmod(vdone[0], W5)
                junk = work.tile([P, D], F32, tag="junk", bufs=3)
                nc.vector.scalar_tensor_tensor(
                    out=junk[:],
                    in0=qb[:, r, :],
                    scalar=1.0,
                    in1=k_v[:, r + j, :],
                    op0=ALU.mult,
                    op1=ALU.mult,
                    accum_out=scv[:, r, j : j + 1],
                )
                vdone[0] += 1
                if vdone[0] == W5 * NV:
                    nc.vector.tensor_tensor(out=scv[:], in0=scv[:], in1=negv[:], op=ALU.add)
                    yv = small.tile([P, NV, W5], F32)
                    softmax(scv, NV, yv[:], "v")
                    nc.sync.dma_start(
                        out=of[VS : VS + P * NV, :].rearrange("(p r) j -> p (r j)", r=NV),
                        in_=yv[:].rearrange("p r j -> p (r j)"),
                    )

        def mxp_group(b, c):
            key = "p%d" % b
            if c == 0:
                qt_sb = qtp.tile([P, 8, S], F32, tag="qt")
                qts[b] = qt_sb
            qt = tp.tile([P, 512], F32, tag="tp")
            for g in range(2):
                nc.tensor.matmul_mx(
                    out=qt[:],
                    lhsT=wc[:, g, P * c : P * (c + 1)].bitcast(FP8X4),
                    lhsT_scale=ws[:, g, P * c : P * (c + 1)],
                    rhs=xc[key][:, g, :].bitcast(FP8X4),
                    rhs_scale=xs[key][:, g, :],
                    start=(g == 0),
                    stop=(g == 1),
                )
            nc.scalar.activation(out=qts[b][:, c, :], in_=qt[:], func=ACT.Identity, bias=bpp[:, c : c + 1], scale=1.0)

        def sc_tile(b, tb):
            if tb % 2 == 0:
                sps = sp.tile([P, 2, NWIN], F32, tag="s")
                spt[b] = sps
            lo = KPAD - 2 + P * tb
            for c in range(8):
                nc.tensor.matmul(
                    out=spt[b][:, tb % 2, :],
                    lhsT=qts[b][:, c, P * tb : P * (tb + 1)],
                    rhs=kts[b][:, c, lo : lo + NWIN],
                    start=(c == 0),
                    stop=(c == 7),
                )

        def ex_half(b, half):
            bm = work.tile([P, 2, NWIN], F32, tag="bm")
            nc.vector.tensor_tensor(
                out=bm[:], in0=spt[b][:], in1=band[:].unsqueeze(1).to_broadcast([P, 2, NWIN]), op=ALU.mult
            )
            slot = 4 * b + 2 * half
            nc.vector.tensor_reduce(
                out=rr[:, slot : slot + 2, 0:MOD],
                in_=bm[:].rearrange("p t (m r) -> p t r m", r=MOD),
                axis=AX.X,
                op=ALU.add,
            )
            pr = work.tile([P, 2, W5, MOD + 1], F32, tag="pr")
            nc.vector.tensor_tensor(
                out=pr[:],
                in0=rr[:, slot : slot + 2, :].unsqueeze(2).to_broadcast([P, 2, W5, MOD + 1]),
                in1=sel[:, 2 * half : 2 * half + 2, :, :],
                op=ALU.mult,
            )
            nc.vector.tensor_reduce(out=sc[:, slot : slot + 2, :], in_=pr[:], axis=AX.X, op=ALU.add)

        for c in range(4):
            w_bank(c, "s")
        w_quant(0)
        for j in range(4):
            x_bank("v0", j, "s")
        x_quant("v0")
        load_xp(PE_BATCHES[-1])
        load_k(PE_BATCHES[-1])
        for c in range(4, 8):
            w_bank(c, "s")
        w_quant(1)
        qb = rawp.tile([P, NV, D], F32, tag="big")
        for vg in range(1, NV // 4):
            for j in range(4):
                x_bank("v%d" % vg, j, "s")
            x_quant("v%d" % vg)
        first = PE_BATCHES[0]
        for r in range(4):
            mxv_group(r, 0)
        for j in range(4):
            x_bank("p%d" % first, j, "s")
        x_quant("p%d" % first)
        for tb in range(4):
            k_bank(first, tb, "s")
        for r in range(4):
            mxv_group(r, 1)
        for r in range(4, NV):
            mxv_group(r, 0)
            mxv_group(r, 1)
        for c in range(8):
            mxp_group(first, c)
        vfill(3)

        for gi, b in enumerate(PE_BATCHES):
            nxt = PE_BATCHES[gi + 1] if gi + 1 < len(PE_BATCHES) else None
            nkey = "p%d" % nxt if nxt is not None else ""
            sc_tile(b, 0)
            if nxt is not None:
                for j in range(3):
                    x_bank(nkey, j, "s")
            vfill(2)
            sc_tile(b, 1)
            if nxt is not None:
                x_bank(nkey, 3, "s")
                k_bank(nxt, 0, "s")
                k_bank(nxt, 1, "s")
                x_quant(nkey)
            ex_half(b, 0)
            vfill(2)
            sc_tile(b, 2)
            if nxt is not None:
                k_bank(nxt, 2, "s")
                k_bank(nxt, 3, "s")
            sc_tile(b, 3)
            ex_half(b, 1)
            if nxt is not None:
                for c in range(8):
                    mxp_group(nxt, c)
                vfill(3)

        softmax(sc, 16, ypad[:, :, 0:16].rearrange("p j t -> p t j"), "p")

        ta = tp.tile([P, 4, P], F32, tag="tp")
        for j in range(4):
            nc.tensor.transpose(ta[:, j, :], ypad[:, j, :], ident[:])
        tb4 = tp.tile([P, 4, P], F32, tag="tp")
        nc.tensor.transpose(tb4[:, 0, :], ypad[:, 4, :], ident[:])
        z2 = small.tile([P, P, W5], F32)
        nc.vector.tensor_copy(out=z2[:, :, 0:4], in_=ta[:].rearrange("s j p -> s p j"))
        nc.vector.tensor_copy(out=z2[:, :, 4:5], in_=tb4[:, 0:1, :].rearrange("s j p -> s p j"))
        ov = of.rearrange("(t p) j -> t (p j)", p=P)
        for b in PE_BATCHES:
            nc.sync.dma_start(out=ov[4 * b : 4 * b + 4, :], in_=z2[4 * b : 4 * b + 4, :, :].rearrange("s p j -> s (p j)"))
        vfill(W5 * NV)
